import numpy as np
import ml_dtypes


def mxq(x, axis, fmt="e4m3"):
    dtype, down = {"e4m3": (ml_dtypes.float8_e4m3fn, 7), "e5m2": (ml_dtypes.float8_e5m2, 14)}[fmt]
    v = np.moveaxis(np.asarray(x, np.float32).astype(ml_dtypes.bfloat16).astype(np.float64), axis, -1)
    blocks = v.reshape(v.shape[:-1] + (-1, 32))
    amax = np.abs(blocks).max(-1, keepdims=True)
    byte = np.maximum(np.where(amax > 0, np.frexp(amax)[1] - 1 + 127, 0) - down, 1)
    scale = np.exp2(byte - 127.0)
    codes = (blocks / scale).astype(np.float32).astype(dtype).astype(np.float64)
    return np.moveaxis((codes * scale).reshape(v.shape), -1, axis)


WIDE = False


def mx_kscale(k):
    if not WIDE:
        return np.ones(k)
    levels = np.array([10, -10, 5, -5, 0])
    a = np.random.permutation(np.resize(levels, k // 512 * 4)).reshape(k // 512, 4)
    idx = np.arange(k)
    return np.exp2(a[idx // 512, idx % 128 // 32])


BF16 = ml_dtypes.bfloat16


def bf(x):
    return np.asarray(x, np.float32).astype(BF16)


def f64(x):
    return np.asarray(x).astype(np.float64)


B, S, H = 4, 1025, 512
N = B * (S - 1)
G = 0.75


def setup_inputs():
    s = mx_kscale(H)
    return {"x": bf(np.random.standard_normal((B, S, H)) * s),
            "k1": bf(np.random.standard_normal((N, H)) * G * s),
            "k2": bf(np.random.standard_normal((N, H)) * G * np.sqrt(1.0 + 0.25 * G * G) * s),
            "coefficients": bf(np.random.standard_normal((H, H)) * G / np.sqrt(H) * s[:, None] / s[None, :])}


def reference(x, k1, k2, coefficients):
    x, k1, k2 = f64(x), f64(k1), f64(k2)
    y = x[:, :-1, :].reshape(-1, H)
    cq = mxq(f64(coefficients), 1, "e4m3")
    k3 = mxq(y + 0.5 * k2, 1, "e4m3") @ cq.T
    k4 = mxq(y + k3, 1, "e4m3") @ cq.T
    y1 = y + (k1 + 2.0 * k2 + 2.0 * k3 + k4) / 6.0
    return y1.reshape(B, S - 1, H) - x[:, 1:, :]

@@ -1,0 +1,214 @@
+from contextlib import ExitStack
+
+import concourse.mybir as mybir
+from concourse.masks import make_identity
+
+F32 = mybir.dt.float32
+BF16 = mybir.dt.bfloat16
+U32 = mybir.dt.uint32
+U8 = mybir.dt.uint8
+FP8X4 = mybir.dt.float8_e4m3fn_x4
+ADD = mybir.AluOpType.add
+SUBTRACT = mybir.AluOpType.subtract
+MULT = mybir.AluOpType.mult
+COPY = mybir.ActivationFunctionType.Copy
+
+P = 128
+H = 512
+PACK = 4
+SEQUENCES = 4
+STEPS = 1024
+STATES_PER_PARTITION = STEPS // P
+UNIT_TILES = 2
+UNIT_ROWS = UNIT_TILES * P
+
+FLOPS = 2 * 2 * SEQUENCES * STEPS * H * H
+
+
+def transpose_unit(nc, psum_turned, identity, row_tiles):
+    turned = psum_turned.tile([P, 2, UNIT_ROWS], F32)
+    for j, rows in enumerate(row_tiles):
+        words = rows.bitcast(F32)
+        for u in range(2):
+            nc.tensor.transpose(
+                turned[:, u, j * P : (j + 1) * P], words[:, u * P : (u + 1) * P], identity[:]
+            )
+    return turned
+
+
+def copy_grouped(nc, grouped, turned):
+    nc.scalar.copy(out=grouped[:].bitcast(F32), in_=turned[:].rearrange("p u m -> p m u"))
+
+
+def quantise(nc, codes, scales, grouped):
+    nc.vector.quantize_mx(
+        out=codes.bitcast(FP8X4), scales=scales, in_=grouped[:].rearrange("p m t -> p (m t)")
+    )
+
+
+def tile_sindylossmixin_pa_t_kernel(tc, x, k1, k2, coefficients, out):
+    nc = tc.nc
+    with ExitStack() as ctx:
+        consts = ctx.enter_context(tc.tile_pool(name="consts", bufs=1))
+        loads = ctx.enter_context(tc.tile_pool(name="loads", bufs=SEQUENCES))
+        work = ctx.enter_context(tc.tile_pool(name="work", bufs=4))
+        psum_turned = ctx.enter_context(tc.psum_pool(name="psum_turned", bufs=3))
+        psum_k3 = ctx.enter_context(tc.psum_pool(name="psum_k3", bufs=2))
+        psum_sum = ctx.enter_context(tc.psum_pool(name="psum_sum", bufs=3))
+
+        identity = consts.tile([P, P], F32)
+        make_identity(nc, identity[:])
+
+        x_sb, k1_sb, k2_sb = [], [], []
+
+        def load_states(s):
+            x_tile = loads.tile([P, STATES_PER_PARTITION + 1, H], BF16)
+            nc.sync.dma_start(
+                out=x_tile[:, 0:STATES_PER_PARTITION, :],
+                in_=x[s, 0:STEPS, :].rearrange("(p t) h -> p t h", t=STATES_PER_PARTITION),
+            )
+            nc.sync.dma_start(
+                out=x_tile[:, STATES_PER_PARTITION : STATES_PER_PARTITION + 1, :],
+                in_=x[s, 1 : STEPS + 1, :].rearrange("(p t) h -> p t h", t=STATES_PER_PARTITION)[
+                    :, STATES_PER_PARTITION - 1 : STATES_PER_PARTITION, :
+                ],
+            )
+            x_sb.append(x_tile)
+
+        def load_stages(s):
+            rows = slice(s * STEPS, (s + 1) * STEPS)
+            k2_tile = loads.tile([P, STATES_PER_PARTITION, H], BF16)
+            nc.sync.dma_start(
+                out=k2_tile[:],
+                in_=k2[rows, :].rearrange("(p t) h -> p t h", t=STATES_PER_PARTITION),
+            )
+            k2_sb.append(k2_tile)
+            k1_tile = loads.tile([P, STATES_PER_PARTITION, H], BF16)
+            nc.sync.dma_start(
+                out=k1_tile[:],
+                in_=k1[rows, :].rearrange("(p t) h -> p t h", t=STATES_PER_PARTITION),
+            )
+            k1_sb.append(k1_tile)
+
+        load_states(0)
+
+        c_rows = consts.tile([P, PACK, H], BF16)
+        c_rows_paired = consts.tile([P, PACK, H], BF16)
+        nc.sync.dma_start(
+            out=c_rows_paired[:].rearrange("p (u e) k -> p u e k", u=2),
+            in_=coefficients.rearrange("(u p e) k -> p u e k", u=2, e=2),
+        )
+        nc.sync.dma_start(out=c_rows[:], in_=coefficients.rearrange("(i p) k -> p i k", p=P))
+
+        load_stages(0)
+        for s in range(1, SEQUENCES):
+            load_states(s)
+            load_stages(s)
+
+        c_codes = consts.tile([P, H], U32, align_bytes=64)
+        c_scales = consts.tile([P, H], U8, align_bytes=64)
+        c_codes_paired = consts.tile([P, H], U32, align_bytes=64)
+        c_scales_paired = consts.tile([P, H], U8, align_bytes=64)
+        for rows_sb, codes, scales in (
+            (c_rows_paired, c_codes_paired, c_scales_paired),
+            (c_rows, c_codes, c_scales),
+        ):
+            for half in range(PACK // UNIT_TILES):
+                cols = slice(half * UNIT_ROWS, (half + 1) * UNIT_ROWS)
+                c_turned = transpose_unit(
+                    nc,
+                    psum_turned,
+                    identity,
+                    [rows_sb[:, half * UNIT_TILES + j, :] for j in range(UNIT_TILES)],
+                )
+                c_grouped = work.tile([P, UNIT_ROWS, PACK], BF16, align_bytes=64)
+                copy_grouped(nc, c_grouped, c_turned)
+                quantise(nc, codes[:, cols], scales[:, cols], c_grouped)
+
+        for s in range(SEQUENCES):
+            out_rows = out[s].rearrange("(p t) h -> p t h", t=STATES_PER_PARTITION)
+            for t0 in range(0, STATES_PER_PARTITION, UNIT_TILES):
+                here = slice(t0, t0 + UNIT_TILES)
+                after = slice(t0 + 1, t0 + 1 + UNIT_TILES)
+
+                rest = work.tile([P, UNIT_TILES, H], F32)
+                nc.vector.tensor_tensor(
+                    out=rest[:], in0=x_sb[s][:, here, :], in1=x_sb[s][:, after, :], op=SUBTRACT
+                )
+                nc.vector.scalar_tensor_tensor(
+                    out=rest[:], in0=k1_sb[s][:, here, :], scalar=1.0 / 6.0, in1=rest[:],
+                    op0=MULT, op1=ADD,
+                )
+                nc.vector.scalar_tensor_tensor(
+                    out=rest[:], in0=k2_sb[s][:, here, :], scalar=1.0 / 3.0, in1=rest[:],
+                    op0=MULT, op1=ADD,
+                )
+
+                half_k2 = work.tile([P, UNIT_TILES, H], BF16)
+                nc.scalar.activation(out=half_k2[:], in_=k2_sb[s][:, here, :], func=COPY, scale=0.5)
+
+                y_turned = transpose_unit(
+                    nc, psum_turned, identity,
+                    [x_sb[s][:, t0 + j, :] for j in range(UNIT_TILES)],
+                )
+                h_turned = transpose_unit(
+                    nc, psum_turned, identity, [half_k2[:, j, :] for j in range(UNIT_TILES)]
+                )
+                y_grouped = work.tile([P, UNIT_ROWS, PACK], BF16, align_bytes=64)
+                copy_grouped(nc, y_grouped, y_turned)
+
+                a_grouped = work.tile([P, UNIT_ROWS, PACK], BF16, align_bytes=64)
+                nc.vector.tensor_tensor(
+                    out=a_grouped[:].rearrange("p m (u e) -> p m u e", u=2),
+                    in0=h_turned[:].bitcast(BF16).rearrange("p u (m e) -> p m u e", e=2),
+                    in1=y_grouped[:].rearrange("p m (u e) -> p m u e", u=2),
+                    op=ADD,
+                )
+                a_codes = work.tile([P, UNIT_ROWS], U32, align_bytes=64)
+                a_scales = work.tile([P, UNIT_ROWS], U8, align_bytes=64)
+                quantise(nc, a_codes[:], a_scales[:], a_grouped)
+
+                b_grouped = work.tile([P, UNIT_ROWS, PACK], BF16, align_bytes=64)
+                for j in range(UNIT_TILES):
+                    tile_rows = slice(j * P, (j + 1) * P)
+                    k3_turned = psum_k3.tile([P, PACK, P], F32)
+                    for t in range(PACK):
+                        tile_cols = slice(t * P, (t + 1) * P)
+                        nc.tensor.matmul_mx(
+                            out=k3_turned[:, t, :],
+                            lhsT=c_codes_paired[:, tile_cols].bitcast(FP8X4),
+                            lhsT_scale=c_scales_paired[:, tile_cols],
+                            rhs=a_codes[:, tile_rows].bitcast(FP8X4),
+                            rhs_scale=a_scales[:, tile_rows],
+                            start=True,
+                            stop=True,
+                        )
+                    nc.vector.tensor_tensor(
+                        out=b_grouped[:, tile_rows, :],
+                        in0=k3_turned[:].rearrange("p t n -> p n t"),
+                        in1=y_grouped[:, tile_rows, :],
+                        op=ADD,
+                    )
+                b_codes = work.tile([P, UNIT_ROWS], U32, align_bytes=64)
+                b_scales = work.tile([P, UNIT_ROWS], U8, align_bytes=64)
+                quantise(nc, b_codes[:], b_scales[:], b_grouped)
+
+                for j in range(UNIT_TILES):
+                    tile_rows = slice(j * P, (j + 1) * P)
+                    stages = psum_sum.tile([P, H], F32)
+                    passes = ((a_codes, a_scales), (a_codes, a_scales), (b_codes, b_scales))
+                    for i, (codes, scales) in enumerate(passes):
+                        nc.tensor.matmul_mx(
+                            out=stages[:],
+                            lhsT=codes[:, tile_rows].bitcast(FP8X4),
+                            lhsT_scale=scales[:, tile_rows],
+                            rhs=c_codes[:].bitcast(FP8X4),
+                            rhs_scale=c_scales[:],
+                            start=(i == 0),
+                            stop=(i == len(passes) - 1),
+                        )
+                    nc.vector.scalar_tensor_tensor(
+                        out=rest[:, j, :], in0=stages[:], scalar=1.0 / 6.0, in1=rest[:, j, :],
+                        op0=MULT, op1=ADD,
+                    )
+                nc.sync.dma_start(out=out_rows[:, here, :], in_=rest[:])

@@ -52,6 +52,7 @@ def tile_sindylossmixin_pa_t_kernel(tc, x, k1, k2, coefficients, out):
         consts = ctx.enter_context(tc.tile_pool(name="consts", bufs=1))
         loads = ctx.enter_context(tc.tile_pool(name="loads", bufs=SEQUENCES))
         work = ctx.enter_context(tc.tile_pool(name="work", bufs=4))
+        sums = ctx.enter_context(tc.tile_pool(name="sums", bufs=8))
         psum_turned = ctx.enter_context(tc.psum_pool(name="psum_turned", bufs=3))
         psum_k3 = ctx.enter_context(tc.psum_pool(name="psum_k3", bufs=2))
         psum_sum = ctx.enter_context(tc.psum_pool(name="psum_sum", bufs=3))
@@ -131,8 +132,8 @@ def tile_sindylossmixin_pa_t_kernel(tc, x, k1, k2, coefficients, out):
                 here = slice(t0, t0 + UNIT_TILES)
                 after = slice(t0 + 1, t0 + 1 + UNIT_TILES)
 
-                rest = work.tile([P, UNIT_TILES, H], F32)
-                nc.vector.tensor_tensor(
+                rest = sums.tile([P, UNIT_TILES, H], F32)
+                nc.gpsimd.tensor_tensor(
                     out=rest[:], in0=x_sb[s][:, here, :], in1=x_sb[s][:, after, :], op=SUBTRACT
                 )
                 nc.vector.scalar_tensor_tensor(

@@ -48,50 +48,20 @@ def quantise(nc, codes, scales, grouped):
 
 def tile_sindylossmixin_pa_t_kernel(tc, x, k1, k2, coefficients, out):
     nc = tc.nc
+    units = [
+        (s, t0) for s in range(SEQUENCES) for t0 in range(0, STATES_PER_PARTITION, UNIT_TILES)
+    ]
     with ExitStack() as ctx:
         consts = ctx.enter_context(tc.tile_pool(name="consts", bufs=1))
         loads = ctx.enter_context(tc.tile_pool(name="loads", bufs=SEQUENCES))
         work = ctx.enter_context(tc.tile_pool(name="work", bufs=4))
-        sums = ctx.enter_context(tc.tile_pool(name="sums", bufs=8))
         psum_turned = ctx.enter_context(tc.psum_pool(name="psum_turned", bufs=3))
         psum_k3 = ctx.enter_context(tc.psum_pool(name="psum_k3", bufs=2))
         psum_sum = ctx.enter_context(tc.psum_pool(name="psum_sum", bufs=3))
+        ctx.enter_context(tc.manual_schedule())
 
         identity = consts.tile([P, P], F32)
         make_identity(nc, identity[:])
-
-        x_sb, k1_sb, k2_sb = [], [], []
-
-        def load_states(s):
-            x_tile = loads.tile([P, STATES_PER_PARTITION + 1, H], BF16)
-            nc.sync.dma_start(
-                out=x_tile[:, 0:STATES_PER_PARTITION, :],
-                in_=x[s, 0:STEPS, :].rearrange("(p t) h -> p t h", t=STATES_PER_PARTITION),
-            )
-            nc.sync.dma_start(
-                out=x_tile[:, STATES_PER_PARTITION : STATES_PER_PARTITION + 1, :],
-                in_=x[s, 1 : STEPS + 1, :].rearrange("(p t) h -> p t h", t=STATES_PER_PARTITION)[
-                    :, STATES_PER_PARTITION - 1 : STATES_PER_PARTITION, :
-                ],
-            )
-            x_sb.append(x_tile)
-
-        def load_stages(s):
-            rows = slice(s * STEPS, (s + 1) * STEPS)
-            k2_tile = loads.tile([P, STATES_PER_PARTITION, H], BF16)
-            nc.sync.dma_start(
-                out=k2_tile[:],
-                in_=k2[rows, :].rearrange("(p t) h -> p t h", t=STATES_PER_PARTITION),
-            )
-            k2_sb.append(k2_tile)
-            k1_tile = loads.tile([P, STATES_PER_PARTITION, H], BF16)
-            nc.sync.dma_start(
-                out=k1_tile[:],
-                in_=k1[rows, :].rearrange("(p t) h -> p t h", t=STATES_PER_PARTITION),
-            )
-            k1_sb.append(k1_tile)
-
-        load_states(0)
 
         c_rows = consts.tile([P, PACK, H], BF16)
         c_rows_paired = consts.tile([P, PACK, H], BF16)
@@ -101,10 +71,38 @@ def tile_sindylossmixin_pa_t_kernel(tc, x, k1, k2, coefficients, out):
         )
         nc.sync.dma_start(out=c_rows[:], in_=coefficients.rearrange("(i p) k -> p i k", p=P))
 
-        load_stages(0)
-        for s in range(1, SEQUENCES):
-            load_states(s)
-            load_stages(s)
+        x_sb, k1_sb, k2_sb = [], [], []
+        for s, t0 in units:
+            here = slice(t0, t0 + UNIT_TILES)
+            after = slice(t0 + 1, t0 + 1 + UNIT_TILES)
+            rows = slice(s * STEPS, (s + 1) * STEPS)
+            if t0 == 0:
+                x_tile = loads.tile([P, STATES_PER_PARTITION + 1, H], BF16)
+                k2_tile = loads.tile([P, STATES_PER_PARTITION, H], BF16)
+                k1_tile = loads.tile([P, STATES_PER_PARTITION, H], BF16)
+                x_sb.append(x_tile)
+                k2_sb.append(k2_tile)
+                k1_sb.append(k1_tile)
+                nc.sync.dma_start(
+                    out=x_tile[:, 0:1, :],
+                    in_=x[s, 0:STEPS, :].rearrange("(p t) h -> p t h", t=STATES_PER_PARTITION)[
+                        :, 0:1, :
+                    ],
+                )
+            nc.sync.dma_start(
+                out=x_sb[s][:, after, :],
+                in_=x[s, 1 : STEPS + 1, :].rearrange("(p t) h -> p t h", t=STATES_PER_PARTITION)[
+                    :, here, :
+                ],
+            )
+            nc.sync.dma_start(
+                out=k2_sb[s][:, here, :],
+                in_=k2[rows, :].rearrange("(p t) h -> p t h", t=STATES_PER_PARTITION)[:, here, :],
+            )
+            nc.sync.dma_start(
+                out=k1_sb[s][:, here, :],
+                in_=k1[rows, :].rearrange("(p t) h -> p t h", t=STATES_PER_PARTITION)[:, here, :],
+            )
 
         c_codes = consts.tile([P, H], U32, align_bytes=64)
         c_scales = consts.tile([P, H], U8, align_bytes=64)
@@ -126,90 +124,148 @@ def tile_sindylossmixin_pa_t_kernel(tc, x, k1, k2, coefficients, out):
                 copy_grouped(nc, c_grouped, c_turned)
                 quantise(nc, codes[:, cols], scales[:, cols], c_grouped)
 
-        for s in range(SEQUENCES):
-            out_rows = out[s].rearrange("(p t) h -> p t h", t=STATES_PER_PARTITION)
-            for t0 in range(0, STATES_PER_PARTITION, UNIT_TILES):
-                here = slice(t0, t0 + UNIT_TILES)
-                after = slice(t0 + 1, t0 + 1 + UNIT_TILES)
+        live = {}
 
-                rest = sums.tile([P, UNIT_TILES, H], F32)
-                nc.gpsimd.tensor_tensor(
-                    out=rest[:], in0=x_sb[s][:, here, :], in1=x_sb[s][:, after, :], op=SUBTRACT
-                )
-                nc.vector.scalar_tensor_tensor(
-                    out=rest[:], in0=k1_sb[s][:, here, :], scalar=1.0 / 6.0, in1=rest[:],
-                    op0=MULT, op1=ADD,
-                )
-                nc.vector.scalar_tensor_tensor(
-                    out=rest[:], in0=k2_sb[s][:, here, :], scalar=1.0 / 3.0, in1=rest[:],
-                    op0=MULT, op1=ADD,
-                )
+        def unit_rows(tiles, i):
+            s, t0 = units[i]
+            return tiles[s][:, t0 : t0 + UNIT_TILES, :]
 
-                half_k2 = work.tile([P, UNIT_TILES, H], BF16)
-                nc.scalar.activation(out=half_k2[:], in_=k2_sb[s][:, here, :], func=COPY, scale=0.5)
+        def turn(i):
+            s, t0 = units[i]
+            half_k2 = work.tile([P, UNIT_TILES, H], BF16)
+            nc.scalar.activation(out=half_k2[:], in_=unit_rows(k2_sb, i), func=COPY, scale=0.5)
+            y_turned = transpose_unit(
+                nc, psum_turned, identity, [x_sb[s][:, t0 + j, :] for j in range(UNIT_TILES)]
+            )
+            h_turned = transpose_unit(
+                nc, psum_turned, identity, [half_k2[:, j, :] for j in range(UNIT_TILES)]
+            )
+            y_grouped = work.tile([P, UNIT_ROWS, PACK], BF16, align_bytes=64)
+            copy_grouped(nc, y_grouped, y_turned)
+            live["h_turned", i] = h_turned
+            live["y_grouped", i] = y_grouped
 
-                y_turned = transpose_unit(
-                    nc, psum_turned, identity,
-                    [x_sb[s][:, t0 + j, :] for j in range(UNIT_TILES)],
-                )
-                h_turned = transpose_unit(
-                    nc, psum_turned, identity, [half_k2[:, j, :] for j in range(UNIT_TILES)]
-                )
-                y_grouped = work.tile([P, UNIT_ROWS, PACK], BF16, align_bytes=64)
-                copy_grouped(nc, y_grouped, y_turned)
+        def rest_difference(i):
+            s, t0 = units[i]
+            rest = work.tile([P, UNIT_TILES, H], F32)
+            nc.vector.tensor_tensor(
+                out=rest[:],
+                in0=x_sb[s][:, t0 : t0 + UNIT_TILES, :],
+                in1=x_sb[s][:, t0 + 1 : t0 + 1 + UNIT_TILES, :],
+                op=SUBTRACT,
+            )
+            live["rest", i] = rest
 
-                a_grouped = work.tile([P, UNIT_ROWS, PACK], BF16, align_bytes=64)
-                nc.vector.tensor_tensor(
-                    out=a_grouped[:].rearrange("p m (u e) -> p m u e", u=2),
-                    in0=h_turned[:].bitcast(BF16).rearrange("p u (m e) -> p m u e", e=2),
-                    in1=y_grouped[:].rearrange("p m (u e) -> p m u e", u=2),
-                    op=ADD,
-                )
-                a_codes = work.tile([P, UNIT_ROWS], U32, align_bytes=64)
-                a_scales = work.tile([P, UNIT_ROWS], U8, align_bytes=64)
-                quantise(nc, a_codes[:], a_scales[:], a_grouped)
+        def rest_add(i, stage_sb, weight):
+            rest = live["rest", i]
+            nc.vector.scalar_tensor_tensor(
+                out=rest[:], in0=unit_rows(stage_sb, i), scalar=weight, in1=rest[:],
+                op0=MULT, op1=ADD,
+            )
 
+        def add_a(i):
+            a_grouped = work.tile([P, UNIT_ROWS, PACK], BF16, align_bytes=64)
+            nc.vector.tensor_tensor(
+                out=a_grouped[:].rearrange("p m (u e) -> p m u e", u=2),
+                in0=live["h_turned", i][:].bitcast(BF16).rearrange("p u (m e) -> p m u e", e=2),
+                in1=live["y_grouped", i][:].rearrange("p m (u e) -> p m u e", u=2),
+                op=ADD,
+            )
+            live["a_grouped", i] = a_grouped
+
+        def quantise_unit(i, operand):
+            codes = work.tile([P, UNIT_ROWS], U32, align_bytes=64, tag=operand + "_codes")
+            scales = work.tile([P, UNIT_ROWS], U8, align_bytes=64, tag=operand + "_scales")
+            quantise(nc, codes[:], scales[:], live[operand + "_grouped", i])
+            live[operand, i] = (codes, scales)
+
+        def first_product(i, j):
+            tile_rows = slice(j * P, (j + 1) * P)
+            a_codes, a_scales = live["a", i]
+            k3_turned = psum_k3.tile([P, PACK, P], F32)
+            for t in range(PACK):
+                tile_cols = slice(t * P, (t + 1) * P)
+                nc.tensor.matmul_mx(
+                    out=k3_turned[:, t, :],
+                    lhsT=c_codes_paired[:, tile_cols].bitcast(FP8X4),
+                    lhsT_scale=c_scales_paired[:, tile_cols],
+                    rhs=a_codes[:, tile_rows].bitcast(FP8X4),
+                    rhs_scale=a_scales[:, tile_rows],
+                    start=True,
+                    stop=True,
+                )
+            live["k3_turned", i, j] = k3_turned
+
+        def add_b(i, j):
+            tile_rows = slice(j * P, (j + 1) * P)
+            if j == 0:
                 b_grouped = work.tile([P, UNIT_ROWS, PACK], BF16, align_bytes=64)
-                for j in range(UNIT_TILES):
-                    tile_rows = slice(j * P, (j + 1) * P)
-                    k3_turned = psum_k3.tile([P, PACK, P], F32)
-                    for t in range(PACK):
-                        tile_cols = slice(t * P, (t + 1) * P)
-                        nc.tensor.matmul_mx(
-                            out=k3_turned[:, t, :],
-                            lhsT=c_codes_paired[:, tile_cols].bitcast(FP8X4),
-                            lhsT_scale=c_scales_paired[:, tile_cols],
-                            rhs=a_codes[:, tile_rows].bitcast(FP8X4),
-                            rhs_scale=a_scales[:, tile_rows],
-                            start=True,
-                            stop=True,
-                        )
-                    nc.vector.tensor_tensor(
-                        out=b_grouped[:, tile_rows, :],
-                        in0=k3_turned[:].rearrange("p t n -> p n t"),
-                        in1=y_grouped[:, tile_rows, :],
-                        op=ADD,
-                    )
-                b_codes = work.tile([P, UNIT_ROWS], U32, align_bytes=64)
-                b_scales = work.tile([P, UNIT_ROWS], U8, align_bytes=64)
-                quantise(nc, b_codes[:], b_scales[:], b_grouped)
+                live["b_grouped", i] = b_grouped
+            nc.vector.tensor_tensor(
+                out=live["b_grouped", i][:, tile_rows, :],
+                in0=live["k3_turned", i, j][:].rearrange("p t n -> p n t"),
+                in1=live["y_grouped", i][:, tile_rows, :],
+                op=ADD,
+            )
 
-                for j in range(UNIT_TILES):
-                    tile_rows = slice(j * P, (j + 1) * P)
-                    stages = psum_sum.tile([P, H], F32)
-                    passes = ((a_codes, a_scales), (a_codes, a_scales), (b_codes, b_scales))
-                    for i, (codes, scales) in enumerate(passes):
-                        nc.tensor.matmul_mx(
-                            out=stages[:],
-                            lhsT=codes[:, tile_rows].bitcast(FP8X4),
-                            lhsT_scale=scales[:, tile_rows],
-                            rhs=c_codes[:].bitcast(FP8X4),
-                            rhs_scale=c_scales[:],
-                            start=(i == 0),
-                            stop=(i == len(passes) - 1),
-                        )
-                    nc.vector.scalar_tensor_tensor(
-                        out=rest[:, j, :], in0=stages[:], scalar=1.0 / 6.0, in1=rest[:, j, :],
-                        op0=MULT, op1=ADD,
-                    )
-                nc.sync.dma_start(out=out_rows[:, here, :], in_=rest[:])
+        def second_product(i, j):
+            tile_rows = slice(j * P, (j + 1) * P)
+            stages = psum_sum.tile([P, H], F32)
+            passes = (live["a", i], live["a", i], live["b", i])
+            for n, (codes, scales) in enumerate(passes):
+                nc.tensor.matmul_mx(
+                    out=stages[:],
+                    lhsT=codes[:, tile_rows].bitcast(FP8X4),
+                    lhsT_scale=scales[:, tile_rows],
+                    rhs=c_codes[:].bitcast(FP8X4),
+                    rhs_scale=c_scales[:],
+                    start=(n == 0),
+                    stop=(n == len(passes) - 1),
+                )
+            live["stages", i, j] = stages
+
+        def finish(i, j):
+            rest = live["rest", i]
+            nc.vector.scalar_tensor_tensor(
+                out=rest[:, j, :], in0=live["stages", i, j][:], scalar=1.0 / 6.0,
+                in1=rest[:, j, :], op0=MULT, op1=ADD,
+            )
+
+        def store(i):
+            s, t0 = units[i]
+            nc.sync.dma_start(
+                out=out[s].rearrange("(p t) h -> p t h", t=STATES_PER_PARTITION)[
+                    :, t0 : t0 + UNIT_TILES, :
+                ],
+                in_=live["rest", i][:],
+            )
+
+        def in_flight(i):
+            return 0 <= i < len(units)
+
+        turn(0)
+        for i in range(len(units) + 2):
+            if in_flight(i + 1):
+                turn(i + 1)
+            if in_flight(i):
+                rest_difference(i)
+                add_a(i)
+            if in_flight(i - 1):
+                add_b(i - 1, 0)
+            if in_flight(i):
+                quantise_unit(i, "a")
+                first_product(i, 0)
+                first_product(i, 1)
+                rest_add(i, k1_sb, 1.0 / 6.0)
+            if in_flight(i - 1):
+                add_b(i - 1, 1)
+            if in_flight(i):
+                rest_add(i, k2_sb, 1.0 / 3.0)
+            if in_flight(i - 1):
+                quantise_unit(i - 1, "b")
+                second_product(i - 1, 0)
+                second_product(i - 1, 1)
+            if in_flight(i - 2):
+                finish(i - 2, 0)
+                finish(i - 2, 1)
+                store(i - 2)

@@ -25,24 +25,28 @@ UNIT_ROWS = UNIT_TILES * P
 FLOPS = 2 * 2 * SEQUENCES * STEPS * H * H
 
 
-def transpose_unit(nc, psum_turned, identity, row_tiles):
-    turned = psum_turned.tile([P, 2, UNIT_ROWS], F32)
-    for j, rows in enumerate(row_tiles):
-        words = rows.bitcast(F32)
-        for u in range(2):
-            nc.tensor.transpose(
-                turned[:, u, j * P : (j + 1) * P], words[:, u * P : (u + 1) * P], identity[:]
+def sum_turned(nc, psum_turned, identity, terms):
+    turned = psum_turned.tile([P, PACK, P], F32)
+    for t in range(PACK):
+        for n, term in enumerate(terms):
+            nc.tensor.matmul(
+                out=turned[:, t, :],
+                lhsT=term[:, t * P : (t + 1) * P],
+                rhs=identity[:],
+                start=(n == 0),
+                stop=(n == len(terms) - 1),
+                is_transpose=True,
             )
     return turned
 
 
-def copy_grouped(nc, grouped, turned):
-    nc.scalar.copy(out=grouped[:].bitcast(F32), in_=turned[:].rearrange("p u m -> p m u"))
+def round_grouped(nc, grouped_rows, turned):
+    nc.scalar.copy(out=grouped_rows, in_=turned[:].rearrange("p t n -> p n t"))
 
 
 def quantise(nc, codes, scales, grouped):
     nc.vector.quantize_mx(
-        out=codes.bitcast(FP8X4), scales=scales, in_=grouped[:].rearrange("p m t -> p (m t)")
+        out=codes[:].bitcast(FP8X4), scales=scales[:], in_=grouped[:].rearrange("p m t -> p (m t)")
     )
 
 
@@ -51,24 +55,20 @@ def tile_sindylossmixin_pa_t_kernel(tc, x, k1, k2, coefficients, out):
     units = [
         (s, t0) for s in range(SEQUENCES) for t0 in range(0, STATES_PER_PARTITION, UNIT_TILES)
     ]
+    tiles = [slice(j * P, (j + 1) * P) for j in range(UNIT_TILES)]
     with ExitStack() as ctx:
         consts = ctx.enter_context(tc.tile_pool(name="consts", bufs=1))
         loads = ctx.enter_context(tc.tile_pool(name="loads", bufs=SEQUENCES))
         work = ctx.enter_context(tc.tile_pool(name="work", bufs=4))
-        psum_turned = ctx.enter_context(tc.psum_pool(name="psum_turned", bufs=3))
+        psum_turned = ctx.enter_context(tc.psum_pool(name="psum_turned", bufs=4))
         psum_k3 = ctx.enter_context(tc.psum_pool(name="psum_k3", bufs=2))
-        psum_sum = ctx.enter_context(tc.psum_pool(name="psum_sum", bufs=3))
+        psum_sum = ctx.enter_context(tc.psum_pool(name="psum_sum", bufs=2))
         ctx.enter_context(tc.manual_schedule())
 
         identity = consts.tile([P, P], F32)
         make_identity(nc, identity[:])
 
         c_rows = consts.tile([P, PACK, H], BF16)
-        c_rows_paired = consts.tile([P, PACK, H], BF16)
-        nc.sync.dma_start(
-            out=c_rows_paired[:].rearrange("p (u e) k -> p u e k", u=2),
-            in_=coefficients.rearrange("(u p e) k -> p u e k", u=2, e=2),
-        )
         nc.sync.dma_start(out=c_rows[:], in_=coefficients.rearrange("(i p) k -> p i k", p=P))
 
         x_sb, k1_sb, k2_sb = [], [], []
@@ -104,46 +104,75 @@ def tile_sindylossmixin_pa_t_kernel(tc, x, k1, k2, coefficients, out):
                 in_=k1[rows, :].rearrange("(p t) h -> p t h", t=STATES_PER_PARTITION)[:, here, :],
             )
 
-        c_codes = consts.tile([P, H], U32, align_bytes=64)
-        c_scales = consts.tile([P, H], U8, align_bytes=64)
-        c_codes_paired = consts.tile([P, H], U32, align_bytes=64)
-        c_scales_paired = consts.tile([P, H], U8, align_bytes=64)
-        for rows_sb, codes, scales in (
-            (c_rows_paired, c_codes_paired, c_scales_paired),
-            (c_rows, c_codes, c_scales),
-        ):
-            for half in range(PACK // UNIT_TILES):
-                cols = slice(half * UNIT_ROWS, (half + 1) * UNIT_ROWS)
-                c_turned = transpose_unit(
+        live = {}
+
+        def unit_rows(tiles_sb, i):
+            s, t0 = units[i]
+            return tiles_sb[s][:, t0 : t0 + UNIT_TILES, :]
+
+        def widen_on_scalar(i):
+            h_wide = work.tile([P, UNIT_TILES, H], F32)
+            nc.scalar.activation(out=h_wide[:], in_=unit_rows(k2_sb, i), func=COPY, scale=0.5)
+            y_wide = work.tile([P, UNIT_TILES, H], F32)
+            nc.scalar.copy(out=y_wide[:, 0, :], in_=unit_rows(x_sb, i)[:, 0, :])
+            live["h_wide", i] = h_wide
+            live["y_wide", i] = y_wide
+
+        def widen_on_vector(i):
+            nc.vector.tensor_copy(out=live["y_wide", i][:, 1, :], in_=unit_rows(x_sb, i)[:, 1, :])
+
+        def turn(i, operand, second_term):
+            for j in range(UNIT_TILES):
+                live[operand + "_turned", i, j] = sum_turned(
                     nc,
                     psum_turned,
                     identity,
-                    [rows_sb[:, half * UNIT_TILES + j, :] for j in range(UNIT_TILES)],
+                    [live["y_wide", i][:, j, :], live[second_term, i][:, j, :]],
                 )
-                c_grouped = work.tile([P, UNIT_ROWS, PACK], BF16, align_bytes=64)
-                copy_grouped(nc, c_grouped, c_turned)
-                quantise(nc, codes[:, cols], scales[:, cols], c_grouped)
 
-        live = {}
+        def round_unit(i, operand):
+            grouped = work.tile([P, UNIT_ROWS, PACK], BF16, align_bytes=64, tag=operand + "_grouped")
+            for j in range(UNIT_TILES):
+                round_grouped(nc, grouped[:, tiles[j], :], live[operand + "_turned", i, j])
+            live[operand + "_grouped", i] = grouped
 
-        def unit_rows(tiles, i):
-            s, t0 = units[i]
-            return tiles[s][:, t0 : t0 + UNIT_TILES, :]
+        def quantise_unit(i, operand):
+            codes = work.tile([P, UNIT_ROWS], U32, align_bytes=64, tag=operand + "_codes")
+            scales = work.tile([P, UNIT_ROWS], U8, align_bytes=64, tag=operand + "_scales")
+            quantise(nc, codes, scales, live[operand + "_grouped", i])
+            live[operand, i] = (codes, scales)
 
-        def turn(i):
-            s, t0 = units[i]
-            half_k2 = work.tile([P, UNIT_TILES, H], BF16)
-            nc.scalar.activation(out=half_k2[:], in_=unit_rows(k2_sb, i), func=COPY, scale=0.5)
-            y_turned = transpose_unit(
-                nc, psum_turned, identity, [x_sb[s][:, t0 + j, :] for j in range(UNIT_TILES)]
+        def product(acc, rows_operand, tile_rows, weight, start, stop):
+            codes, scales = rows_operand
+            c_codes, c_scales = c_operand[weight]
+            nc.tensor.matmul_mx(
+                out=acc[:],
+                lhsT=codes[:, tile_rows].bitcast(FP8X4),
+                lhsT_scale=scales[:, tile_rows],
+                rhs=c_codes[:].bitcast(FP8X4),
+                rhs_scale=c_scales[:],
+                start=start,
+                stop=stop,
             )
-            h_turned = transpose_unit(
-                nc, psum_turned, identity, [half_k2[:, j, :] for j in range(UNIT_TILES)]
-            )
-            y_grouped = work.tile([P, UNIT_ROWS, PACK], BF16, align_bytes=64)
-            copy_grouped(nc, y_grouped, y_turned)
-            live["h_turned", i] = h_turned
-            live["y_grouped", i] = y_grouped
+
+        def first_product(i):
+            for j in range(UNIT_TILES):
+                k3 = psum_k3.tile([P, H], F32)
+                product(k3, live["a", i], tiles[j], 1, True, True)
+                live["k3", i, j] = k3
+
+        def copy_k3(i):
+            k3_wide = work.tile([P, UNIT_TILES, H], F32)
+            for j in range(UNIT_TILES):
+                nc.scalar.copy(out=k3_wide[:, j, :], in_=live["k3", i, j][:])
+            live["k3_wide", i] = k3_wide
+
+        def second_product(i):
+            for j in range(UNIT_TILES):
+                stages = psum_sum.tile([P, H], F32)
+                product(stages, live["a", i], tiles[j], 2, True, False)
+                product(stages, live["b", i], tiles[j], 1, False, True)
+                live["stages", i, j] = stages
 
         def rest_difference(i):
             s, t0 = units[i]
@@ -163,67 +192,6 @@ def tile_sindylossmixin_pa_t_kernel(tc, x, k1, k2, coefficients, out):
                 op0=MULT, op1=ADD,
             )
 
-        def add_a(i):
-            a_grouped = work.tile([P, UNIT_ROWS, PACK], BF16, align_bytes=64)
-            nc.vector.tensor_tensor(
-                out=a_grouped[:].rearrange("p m (u e) -> p m u e", u=2),
-                in0=live["h_turned", i][:].bitcast(BF16).rearrange("p u (m e) -> p m u e", e=2),
-                in1=live["y_grouped", i][:].rearrange("p m (u e) -> p m u e", u=2),
-                op=ADD,
-            )
-            live["a_grouped", i] = a_grouped
-
-        def quantise_unit(i, operand):
-            codes = work.tile([P, UNIT_ROWS], U32, align_bytes=64, tag=operand + "_codes")
-            scales = work.tile([P, UNIT_ROWS], U8, align_bytes=64, tag=operand + "_scales")
-            quantise(nc, codes[:], scales[:], live[operand + "_grouped", i])
-            live[operand, i] = (codes, scales)
-
-        def first_product(i, j):
-            tile_rows = slice(j * P, (j + 1) * P)
-            a_codes, a_scales = live["a", i]
-            k3_turned = psum_k3.tile([P, PACK, P], F32)
-            for t in range(PACK):
-                tile_cols = slice(t * P, (t + 1) * P)
-                nc.tensor.matmul_mx(
-                    out=k3_turned[:, t, :],
-                    lhsT=c_codes_paired[:, tile_cols].bitcast(FP8X4),
-                    lhsT_scale=c_scales_paired[:, tile_cols],
-                    rhs=a_codes[:, tile_rows].bitcast(FP8X4),
-                    rhs_scale=a_scales[:, tile_rows],
-                    start=True,
-                    stop=True,
-                )
-            live["k3_turned", i, j] = k3_turned
-
-        def add_b(i, j):
-            tile_rows = slice(j * P, (j + 1) * P)
-            if j == 0:
-                b_grouped = work.tile([P, UNIT_ROWS, PACK], BF16, align_bytes=64)
-                live["b_grouped", i] = b_grouped
-            nc.vector.tensor_tensor(
-                out=live["b_grouped", i][:, tile_rows, :],
-                in0=live["k3_turned", i, j][:].rearrange("p t n -> p n t"),
-                in1=live["y_grouped", i][:, tile_rows, :],
-                op=ADD,
-            )
-
-        def second_product(i, j):
-            tile_rows = slice(j * P, (j + 1) * P)
-            stages = psum_sum.tile([P, H], F32)
-            passes = (live["a", i], live["a", i], live["b", i])
-            for n, (codes, scales) in enumerate(passes):
-                nc.tensor.matmul_mx(
-                    out=stages[:],
-                    lhsT=codes[:, tile_rows].bitcast(FP8X4),
-                    lhsT_scale=scales[:, tile_rows],
-                    rhs=c_codes[:].bitcast(FP8X4),
-                    rhs_scale=c_scales[:],
-                    start=(n == 0),
-                    stop=(n == len(passes) - 1),
-                )
-            live["stages", i, j] = stages
-
         def finish(i, j):
             rest = live["rest", i]
             nc.vector.scalar_tensor_tensor(
@@ -240,32 +208,53 @@ def tile_sindylossmixin_pa_t_kernel(tc, x, k1, k2, coefficients, out):
                 in_=live["rest", i][:],
             )
 
+        c_wide = consts.tile([P, PACK, H], F32)
+        nc.vector.tensor_copy(out=c_wide[:], in_=c_rows[:])
+        widen_on_scalar(0)
+        widen_on_vector(0)
+        c_grouped = consts.tile([P, H, PACK], BF16, align_bytes=64)
+        for i in range(PACK):
+            c_turned = sum_turned(nc, psum_turned, identity, [c_wide[:, i, :]])
+            nc.vector.tensor_copy(
+                out=c_grouped[:, i * P : (i + 1) * P, :], in_=c_turned[:].rearrange("p t n -> p n t")
+            )
+        c_doubled = consts.tile([P, H, PACK], BF16, align_bytes=64)
+        nc.vector.tensor_scalar_mul(out=c_doubled[:], in0=c_grouped[:], scalar1=2.0)
+        c_operand = {}
+        for weight, grouped in ((1, c_grouped), (2, c_doubled)):
+            c_codes = consts.tile([P, H], U32, align_bytes=64, tag="c_codes%d" % weight)
+            c_scales = consts.tile([P, H], U8, align_bytes=64, tag="c_scales%d" % weight)
+            quantise(nc, c_codes, c_scales, grouped)
+            c_operand[weight] = (c_codes, c_scales)
+
         def in_flight(i):
             return 0 <= i < len(units)
 
-        turn(0)
-        for i in range(len(units) + 2):
-            if in_flight(i + 1):
-                turn(i + 1)
-            if in_flight(i):
-                rest_difference(i)
-                add_a(i)
-            if in_flight(i - 1):
-                add_b(i - 1, 0)
-            if in_flight(i):
-                quantise_unit(i, "a")
-                first_product(i, 0)
-                first_product(i, 1)
-                rest_add(i, k1_sb, 1.0 / 6.0)
-            if in_flight(i - 1):
-                add_b(i - 1, 1)
-            if in_flight(i):
-                rest_add(i, k2_sb, 1.0 / 3.0)
-            if in_flight(i - 1):
-                quantise_unit(i - 1, "b")
-                second_product(i - 1, 0)
-                second_product(i - 1, 1)
-            if in_flight(i - 2):
-                finish(i - 2, 0)
-                finish(i - 2, 1)
-                store(i - 2)
+        for r in range(len(units) + 2):
+            if in_flight(r):
+                turn(r, "a", "h_wide")
+            if in_flight(r - 1):
+                copy_k3(r - 1)
+                turn(r - 1, "b", "k3_wide")
+            if in_flight(r):
+                rest_difference(r)
+            if in_flight(r - 2):
+                quantise_unit(r - 2, "b")
+                second_product(r - 2)
+            if in_flight(r):
+                round_unit(r, "a")
+                rest_add(r, k1_sb, 1.0 / 6.0)
+                quantise_unit(r, "a")
+                first_product(r)
+            if in_flight(r - 1):
+                round_unit(r - 1, "b")
+            if in_flight(r + 1):
+                widen_on_scalar(r + 1)
+            if in_flight(r):
+                rest_add(r, k2_sb, 1.0 / 3.0)
+            if in_flight(r + 1):
+                widen_on_vector(r + 1)
+            if in_flight(r - 2):
+                finish(r - 2, 0)
+                finish(r - 2, 1)
+                store(r - 2)

@@ -25,23 +25,23 @@ UNIT_ROWS = UNIT_TILES * P
 FLOPS = 2 * 2 * SEQUENCES * STEPS * H * H
 
 
-def sum_turned(nc, psum_turned, identity, terms):
-    turned = psum_turned.tile([P, PACK, P], F32)
-    for t in range(PACK):
-        for n, term in enumerate(terms):
-            nc.tensor.matmul(
-                out=turned[:, t, :],
-                lhsT=term[:, t * P : (t + 1) * P],
-                rhs=identity[:],
-                start=(n == 0),
-                stop=(n == len(terms) - 1),
-                is_transpose=True,
+def transpose_pairs(nc, psum_pairs, identity, row_tiles):
+    turned = psum_pairs.tile([P, 2, UNIT_ROWS], F32)
+    for j, rows in enumerate(row_tiles):
+        words = rows.bitcast(F32)
+        for u in range(2):
+            nc.tensor.transpose(
+                turned[:, u, j * P : (j + 1) * P], words[:, u * P : (u + 1) * P], identity[:]
             )
     return turned
 
 
-def round_grouped(nc, grouped_rows, turned):
-    nc.scalar.copy(out=grouped_rows, in_=turned[:].rearrange("p t n -> p n t"))
+def copy_pairs(nc, grouped, turned):
+    nc.scalar.copy(out=grouped[:].bitcast(F32), in_=turned[:].rearrange("p u m -> p m u"))
+
+
+def by_word_value(row):
+    return row.rearrange("p (u q e) -> p u e q", u=2, e=2)
 
 
 def quantise(nc, codes, scales, grouped):
@@ -52,18 +52,14 @@ def quantise(nc, codes, scales, grouped):
 
 def tile_sindylossmixin_pa_t_kernel(tc, x, k1, k2, coefficients, out):
     nc = tc.nc
-    units = [
-        (s, t0) for s in range(SEQUENCES) for t0 in range(0, STATES_PER_PARTITION, UNIT_TILES)
-    ]
-    tiles = [slice(j * P, (j + 1) * P) for j in range(UNIT_TILES)]
     with ExitStack() as ctx:
         consts = ctx.enter_context(tc.tile_pool(name="consts", bufs=1))
         loads = ctx.enter_context(tc.tile_pool(name="loads", bufs=SEQUENCES))
         work = ctx.enter_context(tc.tile_pool(name="work", bufs=4))
-        psum_turned = ctx.enter_context(tc.psum_pool(name="psum_turned", bufs=4))
+        psum_pairs = ctx.enter_context(tc.psum_pool(name="psum_pairs", bufs=2))
+        psum_b = ctx.enter_context(tc.psum_pool(name="psum_b", bufs=2))
         psum_k3 = ctx.enter_context(tc.psum_pool(name="psum_k3", bufs=2))
         psum_sum = ctx.enter_context(tc.psum_pool(name="psum_sum", bufs=2))
-        ctx.enter_context(tc.manual_schedule())
 
         identity = consts.tile([P, P], F32)
         make_identity(nc, identity[:])
@@ -72,75 +68,48 @@ def tile_sindylossmixin_pa_t_kernel(tc, x, k1, k2, coefficients, out):
         nc.sync.dma_start(out=c_rows[:], in_=coefficients.rearrange("(i p) k -> p i k", p=P))
 
         x_sb, k1_sb, k2_sb = [], [], []
-        for s, t0 in units:
-            here = slice(t0, t0 + UNIT_TILES)
-            after = slice(t0 + 1, t0 + 1 + UNIT_TILES)
+        for s in range(SEQUENCES):
             rows = slice(s * STEPS, (s + 1) * STEPS)
-            if t0 == 0:
-                x_tile = loads.tile([P, STATES_PER_PARTITION + 1, H], BF16)
-                k2_tile = loads.tile([P, STATES_PER_PARTITION, H], BF16)
-                k1_tile = loads.tile([P, STATES_PER_PARTITION, H], BF16)
-                x_sb.append(x_tile)
-                k2_sb.append(k2_tile)
-                k1_sb.append(k1_tile)
-                nc.sync.dma_start(
-                    out=x_tile[:, 0:1, :],
-                    in_=x[s, 0:STEPS, :].rearrange("(p t) h -> p t h", t=STATES_PER_PARTITION)[
-                        :, 0:1, :
-                    ],
-                )
+            x_tile = loads.tile([P, STATES_PER_PARTITION + 1, H], BF16)
             nc.sync.dma_start(
-                out=x_sb[s][:, after, :],
+                out=x_tile[:, 0:STATES_PER_PARTITION, :],
+                in_=x[s, 0:STEPS, :].rearrange("(p t) h -> p t h", t=STATES_PER_PARTITION),
+            )
+            nc.sync.dma_start(
+                out=x_tile[:, STATES_PER_PARTITION : STATES_PER_PARTITION + 1, :],
                 in_=x[s, 1 : STEPS + 1, :].rearrange("(p t) h -> p t h", t=STATES_PER_PARTITION)[
-                    :, here, :
+                    :, STATES_PER_PARTITION - 1 : STATES_PER_PARTITION, :
                 ],
             )
+            x_sb.append(x_tile)
+            k2_tile = loads.tile([P, STATES_PER_PARTITION, H], BF16)
             nc.sync.dma_start(
-                out=k2_sb[s][:, here, :],
-                in_=k2[rows, :].rearrange("(p t) h -> p t h", t=STATES_PER_PARTITION)[:, here, :],
+                out=k2_tile[:],
+                in_=k2[rows, :].rearrange("(p t) h -> p t h", t=STATES_PER_PARTITION),
             )
+            k2_sb.append(k2_tile)
+            k1_tile = loads.tile([P, STATES_PER_PARTITION, H], BF16)
             nc.sync.dma_start(
-                out=k1_sb[s][:, here, :],
-                in_=k1[rows, :].rearrange("(p t) h -> p t h", t=STATES_PER_PARTITION)[:, here, :],
+                out=k1_tile[:],
+                in_=k1[rows, :].rearrange("(p t) h -> p t h", t=STATES_PER_PARTITION),
             )
+            k1_sb.append(k1_tile)
 
-        live = {}
-
-        def unit_rows(tiles_sb, i):
-            s, t0 = units[i]
-            return tiles_sb[s][:, t0 : t0 + UNIT_TILES, :]
-
-        def widen_on_scalar(i):
-            h_wide = work.tile([P, UNIT_TILES, H], F32)
-            nc.scalar.activation(out=h_wide[:], in_=unit_rows(k2_sb, i), func=COPY, scale=0.5)
-            y_wide = work.tile([P, UNIT_TILES, H], F32)
-            nc.scalar.copy(out=y_wide[:, 0, :], in_=unit_rows(x_sb, i)[:, 0, :])
-            live["h_wide", i] = h_wide
-            live["y_wide", i] = y_wide
-
-        def widen_on_vector(i):
-            nc.vector.tensor_copy(out=live["y_wide", i][:, 1, :], in_=unit_rows(x_sb, i)[:, 1, :])
-
-        def turn(i, operand, second_term):
-            for j in range(UNIT_TILES):
-                live[operand + "_turned", i, j] = sum_turned(
-                    nc,
-                    psum_turned,
-                    identity,
-                    [live["y_wide", i][:, j, :], live[second_term, i][:, j, :]],
-                )
-
-        def round_unit(i, operand):
-            grouped = work.tile([P, UNIT_ROWS, PACK], BF16, align_bytes=64, tag=operand + "_grouped")
-            for j in range(UNIT_TILES):
-                round_grouped(nc, grouped[:, tiles[j], :], live[operand + "_turned", i, j])
-            live[operand + "_grouped", i] = grouped
-
-        def quantise_unit(i, operand):
-            codes = work.tile([P, UNIT_ROWS], U32, align_bytes=64, tag=operand + "_codes")
-            scales = work.tile([P, UNIT_ROWS], U8, align_bytes=64, tag=operand + "_scales")
-            quantise(nc, codes, scales, live[operand + "_grouped", i])
-            live[operand, i] = (codes, scales)
+        c_grouped = consts.tile([P, H, PACK], BF16, align_bytes=64)
+        for half in range(PACK // UNIT_TILES):
+            c_turned = transpose_pairs(
+                nc, psum_pairs, identity,
+                [c_rows[:, half * UNIT_TILES + j, :] for j in range(UNIT_TILES)],
+            )
+            copy_pairs(nc, c_grouped[:, half * UNIT_ROWS : (half + 1) * UNIT_ROWS, :], c_turned)
+        c_doubled = consts.tile([P, H, PACK], BF16, align_bytes=64)
+        nc.vector.tensor_scalar_mul(out=c_doubled[:], in0=c_grouped[:], scalar1=2.0)
+        c_operand = {}
+        for weight, grouped in ((1, c_grouped), (2, c_doubled)):
+            c_codes = consts.tile([P, H], U32, align_bytes=64, tag="c_codes%d" % weight)
+            c_scales = consts.tile([P, H], U8, align_bytes=64, tag="c_scales%d" % weight)
+            quantise(nc, c_codes, c_scales, grouped)
+            c_operand[weight] = (c_codes, c_scales)
 
         def product(acc, rows_operand, tile_rows, weight, start, stop):
             codes, scales = rows_operand
@@ -155,106 +124,86 @@ def tile_sindylossmixin_pa_t_kernel(tc, x, k1, k2, coefficients, out):
                 stop=stop,
             )
 
-        def first_product(i):
-            for j in range(UNIT_TILES):
-                k3 = psum_k3.tile([P, H], F32)
-                product(k3, live["a", i], tiles[j], 1, True, True)
-                live["k3", i, j] = k3
+        for s in range(SEQUENCES):
+            out_rows = out[s].rearrange("(p t) h -> p t h", t=STATES_PER_PARTITION)
+            for t0 in range(0, STATES_PER_PARTITION, UNIT_TILES):
+                here = slice(t0, t0 + UNIT_TILES)
+                after = slice(t0 + 1, t0 + 1 + UNIT_TILES)
+                tiles = [slice(j * P, (j + 1) * P) for j in range(UNIT_TILES)]
 
-        def copy_k3(i):
-            k3_wide = work.tile([P, UNIT_TILES, H], F32)
-            for j in range(UNIT_TILES):
-                nc.scalar.copy(out=k3_wide[:, j, :], in_=live["k3", i, j][:])
-            live["k3_wide", i] = k3_wide
+                rest = work.tile([P, UNIT_TILES, H], F32)
+                nc.vector.tensor_tensor(
+                    out=rest[:], in0=x_sb[s][:, here, :], in1=x_sb[s][:, after, :], op=SUBTRACT
+                )
+                nc.vector.scalar_tensor_tensor(
+                    out=rest[:], in0=k1_sb[s][:, here, :], scalar=1.0 / 6.0, in1=rest[:],
+                    op0=MULT, op1=ADD,
+                )
+                nc.vector.scalar_tensor_tensor(
+                    out=rest[:], in0=k2_sb[s][:, here, :], scalar=1.0 / 3.0, in1=rest[:],
+                    op0=MULT, op1=ADD,
+                )
 
-        def second_product(i):
-            for j in range(UNIT_TILES):
-                stages = psum_sum.tile([P, H], F32)
-                product(stages, live["a", i], tiles[j], 2, True, False)
-                product(stages, live["b", i], tiles[j], 1, False, True)
-                live["stages", i, j] = stages
+                half_k2 = work.tile([P, UNIT_TILES, H], BF16)
+                nc.scalar.activation(out=half_k2[:], in_=k2_sb[s][:, here, :], func=COPY, scale=0.5)
+                y_turned = transpose_pairs(
+                    nc, psum_pairs, identity, [x_sb[s][:, t0 + j, :] for j in range(UNIT_TILES)]
+                )
+                h_turned = transpose_pairs(
+                    nc, psum_pairs, identity, [half_k2[:, j, :] for j in range(UNIT_TILES)]
+                )
+                y_grouped = work.tile([P, UNIT_ROWS, PACK], BF16, align_bytes=64)
+                copy_pairs(nc, y_grouped, y_turned)
+                a_grouped = work.tile([P, UNIT_ROWS, PACK], BF16, align_bytes=64)
+                nc.vector.tensor_tensor(
+                    out=a_grouped[:].rearrange("p m (u e) -> p m u e", u=2),
+                    in0=h_turned[:].bitcast(BF16).rearrange("p u (m e) -> p m u e", e=2),
+                    in1=y_grouped[:].rearrange("p m (u e) -> p m u e", u=2),
+                    op=ADD,
+                )
+                a_codes = work.tile([P, UNIT_ROWS], U32, align_bytes=64)
+                a_scales = work.tile([P, UNIT_ROWS], U8, align_bytes=64)
+                quantise(nc, a_codes, a_scales, a_grouped)
 
-        def rest_difference(i):
-            s, t0 = units[i]
-            rest = work.tile([P, UNIT_TILES, H], F32)
-            nc.vector.tensor_tensor(
-                out=rest[:],
-                in0=x_sb[s][:, t0 : t0 + UNIT_TILES, :],
-                in1=x_sb[s][:, t0 + 1 : t0 + 1 + UNIT_TILES, :],
-                op=SUBTRACT,
-            )
-            live["rest", i] = rest
+                y_wide = work.tile([P, UNIT_TILES, PACK, P], F32)
+                k3_wide = work.tile([P, UNIT_TILES, PACK, P], F32)
+                b_grouped = work.tile([P, UNIT_ROWS, PACK], BF16, align_bytes=64)
+                for j in range(UNIT_TILES):
+                    nc.scalar.copy(
+                        out=y_wide[:, j, :, :].rearrange("p (u e) q -> p u e q", u=2),
+                        in_=by_word_value(x_sb[s][:, t0 + j, :]),
+                    )
+                    k3 = psum_k3.tile([P, H], F32)
+                    product(k3, (a_codes, a_scales), tiles[j], 1, True, True)
+                    nc.scalar.copy(
+                        out=k3_wide[:, j, :, :].rearrange("p (u e) q -> p u e q", u=2),
+                        in_=by_word_value(k3[:]),
+                    )
+                for j in range(UNIT_TILES):
+                    b_turned = psum_b.tile([P, PACK, P], F32)
+                    for t in range(PACK):
+                        for term, first in ((y_wide, True), (k3_wide, False)):
+                            nc.tensor.matmul(
+                                out=b_turned[:, t, :],
+                                lhsT=term[:, j, t, :],
+                                rhs=identity[:],
+                                start=first,
+                                stop=not first,
+                                is_transpose=True,
+                            )
+                    nc.scalar.copy(
+                        out=b_grouped[:, tiles[j], :], in_=b_turned[:].rearrange("p t n -> p n t")
+                    )
+                b_codes = work.tile([P, UNIT_ROWS], U32, align_bytes=64)
+                b_scales = work.tile([P, UNIT_ROWS], U8, align_bytes=64)
+                quantise(nc, b_codes, b_scales, b_grouped)
 
-        def rest_add(i, stage_sb, weight):
-            rest = live["rest", i]
-            nc.vector.scalar_tensor_tensor(
-                out=rest[:], in0=unit_rows(stage_sb, i), scalar=weight, in1=rest[:],
-                op0=MULT, op1=ADD,
-            )
-
-        def finish(i, j):
-            rest = live["rest", i]
-            nc.vector.scalar_tensor_tensor(
-                out=rest[:, j, :], in0=live["stages", i, j][:], scalar=1.0 / 6.0,
-                in1=rest[:, j, :], op0=MULT, op1=ADD,
-            )
-
-        def store(i):
-            s, t0 = units[i]
-            nc.sync.dma_start(
-                out=out[s].rearrange("(p t) h -> p t h", t=STATES_PER_PARTITION)[
-                    :, t0 : t0 + UNIT_TILES, :
-                ],
-                in_=live["rest", i][:],
-            )
-
-        c_wide = consts.tile([P, PACK, H], F32)
-        nc.vector.tensor_copy(out=c_wide[:], in_=c_rows[:])
-        widen_on_scalar(0)
-        widen_on_vector(0)
-        c_grouped = consts.tile([P, H, PACK], BF16, align_bytes=64)
-        for i in range(PACK):
-            c_turned = sum_turned(nc, psum_turned, identity, [c_wide[:, i, :]])
-            nc.vector.tensor_copy(
-                out=c_grouped[:, i * P : (i + 1) * P, :], in_=c_turned[:].rearrange("p t n -> p n t")
-            )
-        c_doubled = consts.tile([P, H, PACK], BF16, align_bytes=64)
-        nc.vector.tensor_scalar_mul(out=c_doubled[:], in0=c_grouped[:], scalar1=2.0)
-        c_operand = {}
-        for weight, grouped in ((1, c_grouped), (2, c_doubled)):
-            c_codes = consts.tile([P, H], U32, align_bytes=64, tag="c_codes%d" % weight)
-            c_scales = consts.tile([P, H], U8, align_bytes=64, tag="c_scales%d" % weight)
-            quantise(nc, c_codes, c_scales, grouped)
-            c_operand[weight] = (c_codes, c_scales)
-
-        def in_flight(i):
-            return 0 <= i < len(units)
-
-        for r in range(len(units) + 2):
-            if in_flight(r):
-                turn(r, "a", "h_wide")
-            if in_flight(r - 1):
-                copy_k3(r - 1)
-                turn(r - 1, "b", "k3_wide")
-            if in_flight(r):
-                rest_difference(r)
-            if in_flight(r - 2):
-                quantise_unit(r - 2, "b")
-                second_product(r - 2)
-            if in_flight(r):
-                round_unit(r, "a")
-                rest_add(r, k1_sb, 1.0 / 6.0)
-                quantise_unit(r, "a")
-                first_product(r)
-            if in_flight(r - 1):
-                round_unit(r - 1, "b")
-            if in_flight(r + 1):
-                widen_on_scalar(r + 1)
-            if in_flight(r):
-                rest_add(r, k2_sb, 1.0 / 3.0)
-            if in_flight(r + 1):
-                widen_on_vector(r + 1)
-            if in_flight(r - 2):
-                finish(r - 2, 0)
-                finish(r - 2, 1)
-                store(r - 2)
+                for j in range(UNIT_TILES):
+                    stages = psum_sum.tile([P, H], F32)
+                    product(stages, (a_codes, a_scales), tiles[j], 2, True, False)
+                    product(stages, (b_codes, b_scales), tiles[j], 1, False, True)
+                    nc.vector.scalar_tensor_tensor(
+                        out=rest[:, j, :], in0=stages[:], scalar=1.0 / 6.0, in1=rest[:, j, :],
+                        op0=MULT, op1=ADD,
+                    )
+                nc.sync.dma_start(out=out_rows[:, here, :], in_=rest[:])

@@ -52,64 +52,118 @@ def quantise(nc, codes, scales, grouped):
 
 def tile_sindylossmixin_pa_t_kernel(tc, x, k1, k2, coefficients, out):
     nc = tc.nc
+    units = [
+        (s, t0) for s in range(SEQUENCES) for t0 in range(0, STATES_PER_PARTITION, UNIT_TILES)
+    ]
+    tiles = [slice(j * P, (j + 1) * P) for j in range(UNIT_TILES)]
     with ExitStack() as ctx:
         consts = ctx.enter_context(tc.tile_pool(name="consts", bufs=1))
         loads = ctx.enter_context(tc.tile_pool(name="loads", bufs=SEQUENCES))
-        work = ctx.enter_context(tc.tile_pool(name="work", bufs=4))
+        work = ctx.enter_context(tc.tile_pool(name="work", bufs=3))
+        lasting = ctx.enter_context(tc.tile_pool(name="lasting", bufs=5))
         psum_pairs = ctx.enter_context(tc.psum_pool(name="psum_pairs", bufs=2))
         psum_b = ctx.enter_context(tc.psum_pool(name="psum_b", bufs=2))
         psum_k3 = ctx.enter_context(tc.psum_pool(name="psum_k3", bufs=2))
         psum_sum = ctx.enter_context(tc.psum_pool(name="psum_sum", bufs=2))
+        ctx.enter_context(tc.manual_schedule())
 
         identity = consts.tile([P, P], F32)
         make_identity(nc, identity[:])
 
-        c_rows = consts.tile([P, PACK, H], BF16)
-        nc.sync.dma_start(out=c_rows[:], in_=coefficients.rearrange("(i p) k -> p i k", p=P))
-
         x_sb, k1_sb, k2_sb = [], [], []
-        for s in range(SEQUENCES):
+
+        def load_unit(i):
+            s, t0 = units[i]
+            here = slice(t0, t0 + UNIT_TILES)
+            after = slice(t0 + 1, t0 + 1 + UNIT_TILES)
             rows = slice(s * STEPS, (s + 1) * STEPS)
-            x_tile = loads.tile([P, STATES_PER_PARTITION + 1, H], BF16)
+            if t0 == 0:
+                x_tile = loads.tile([P, STATES_PER_PARTITION + 1, H], BF16)
+                k2_tile = loads.tile([P, STATES_PER_PARTITION, H], BF16)
+                k1_tile = loads.tile([P, STATES_PER_PARTITION, H], BF16)
+                x_sb.append(x_tile)
+                k2_sb.append(k2_tile)
+                k1_sb.append(k1_tile)
+                nc.sync.dma_start(
+                    out=x_tile[:, 0:1, :],
+                    in_=x[s, 0:STEPS, :].rearrange("(p t) h -> p t h", t=STATES_PER_PARTITION)[
+                        :, 0:1, :
+                    ],
+                )
             nc.sync.dma_start(
-                out=x_tile[:, 0:STATES_PER_PARTITION, :],
-                in_=x[s, 0:STEPS, :].rearrange("(p t) h -> p t h", t=STATES_PER_PARTITION),
-            )
-            nc.sync.dma_start(
-                out=x_tile[:, STATES_PER_PARTITION : STATES_PER_PARTITION + 1, :],
+                out=x_sb[s][:, after, :],
                 in_=x[s, 1 : STEPS + 1, :].rearrange("(p t) h -> p t h", t=STATES_PER_PARTITION)[
-                    :, STATES_PER_PARTITION - 1 : STATES_PER_PARTITION, :
+                    :, here, :
                 ],
             )
-            x_sb.append(x_tile)
-            k2_tile = loads.tile([P, STATES_PER_PARTITION, H], BF16)
             nc.sync.dma_start(
-                out=k2_tile[:],
-                in_=k2[rows, :].rearrange("(p t) h -> p t h", t=STATES_PER_PARTITION),
+                out=k2_sb[s][:, here, :],
+                in_=k2[rows, :].rearrange("(p t) h -> p t h", t=STATES_PER_PARTITION)[:, here, :],
             )
-            k2_sb.append(k2_tile)
-            k1_tile = loads.tile([P, STATES_PER_PARTITION, H], BF16)
             nc.sync.dma_start(
-                out=k1_tile[:],
-                in_=k1[rows, :].rearrange("(p t) h -> p t h", t=STATES_PER_PARTITION),
+                out=k1_sb[s][:, here, :],
+                in_=k1[rows, :].rearrange("(p t) h -> p t h", t=STATES_PER_PARTITION)[:, here, :],
             )
-            k1_sb.append(k1_tile)
+
+        load_unit(0)
+        c_rows = consts.tile([P, PACK, H], BF16)
+        nc.sync.dma_start(out=c_rows[:], in_=coefficients.rearrange("(i p) k -> p i k", p=P))
+        for i in range(1, len(units)):
+            load_unit(i)
 
         c_grouped = consts.tile([P, H, PACK], BF16, align_bytes=64)
-        for half in range(PACK // UNIT_TILES):
-            c_turned = transpose_pairs(
-                nc, psum_pairs, identity,
-                [c_rows[:, half * UNIT_TILES + j, :] for j in range(UNIT_TILES)],
-            )
-            copy_pairs(nc, c_grouped[:, half * UNIT_ROWS : (half + 1) * UNIT_ROWS, :], c_turned)
         c_doubled = consts.tile([P, H, PACK], BF16, align_bytes=64)
-        nc.vector.tensor_scalar_mul(out=c_doubled[:], in0=c_grouped[:], scalar1=2.0)
         c_operand = {}
-        for weight, grouped in ((1, c_grouped), (2, c_doubled)):
-            c_codes = consts.tile([P, H], U32, align_bytes=64, tag="c_codes%d" % weight)
-            c_scales = consts.tile([P, H], U8, align_bytes=64, tag="c_scales%d" % weight)
-            quantise(nc, c_codes, c_scales, grouped)
-            c_operand[weight] = (c_codes, c_scales)
+
+        def turn_coefficients():
+            for half in range(PACK // UNIT_TILES):
+                c_turned = transpose_pairs(
+                    nc, psum_pairs, identity,
+                    [c_rows[:, half * UNIT_TILES + j, :] for j in range(UNIT_TILES)],
+                )
+                copy_pairs(nc, c_grouped[:, half * UNIT_ROWS : (half + 1) * UNIT_ROWS, :], c_turned)
+
+        def quantise_coefficients():
+            nc.vector.tensor_scalar_mul(out=c_doubled[:], in0=c_grouped[:], scalar1=2.0)
+            for weight, grouped in ((1, c_grouped), (2, c_doubled)):
+                c_codes = consts.tile([P, H], U32, align_bytes=64, tag="c_codes%d" % weight)
+                c_scales = consts.tile([P, H], U8, align_bytes=64, tag="c_scales%d" % weight)
+                quantise(nc, c_codes, c_scales, grouped)
+                c_operand[weight] = (c_codes, c_scales)
+
+        live = {}
+
+        def unit_rows(tiles_sb, i):
+            s, t0 = units[i]
+            return tiles_sb[s][:, t0 : t0 + UNIT_TILES, :]
+
+        def halve_k2(i):
+            half_k2 = work.tile([P, UNIT_TILES, H], BF16)
+            nc.scalar.activation(out=half_k2[:], in_=unit_rows(k2_sb, i), func=COPY, scale=0.5)
+            live["half_k2", i] = half_k2
+
+        def add_a(i):
+            a_rows = work.tile([P, UNIT_TILES, H], BF16)
+            nc.vector.tensor_tensor(
+                out=a_rows[:], in0=unit_rows(x_sb, i), in1=live["half_k2", i][:], op=ADD
+            )
+            live["a_rows", i] = a_rows
+
+        def turn_a(i):
+            live["a_turned", i] = transpose_pairs(
+                nc, psum_pairs, identity, [live["a_rows", i][:, j, :] for j in range(UNIT_TILES)]
+            )
+
+        def copy_a(i):
+            a_grouped = work.tile([P, UNIT_ROWS, PACK], BF16, align_bytes=64)
+            copy_pairs(nc, a_grouped, live["a_turned", i])
+            live["a_grouped", i] = a_grouped
+
+        def quantise_unit(i, operand):
+            codes = lasting.tile([P, UNIT_ROWS], U32, align_bytes=64, tag=operand + "_codes")
+            scales = lasting.tile([P, UNIT_ROWS], U8, align_bytes=64, tag=operand + "_scales")
+            quantise(nc, codes, scales, live[operand + "_grouped", i])
+            live[operand, i] = (codes, scales)
 
         def product(acc, rows_operand, tile_rows, weight, start, stop):
             codes, scales = rows_operand
@@ -124,86 +178,130 @@ def tile_sindylossmixin_pa_t_kernel(tc, x, k1, k2, coefficients, out):
                 stop=stop,
             )
 
-        for s in range(SEQUENCES):
-            out_rows = out[s].rearrange("(p t) h -> p t h", t=STATES_PER_PARTITION)
-            for t0 in range(0, STATES_PER_PARTITION, UNIT_TILES):
-                here = slice(t0, t0 + UNIT_TILES)
-                after = slice(t0 + 1, t0 + 1 + UNIT_TILES)
-                tiles = [slice(j * P, (j + 1) * P) for j in range(UNIT_TILES)]
+        def first_product(i):
+            for j in range(UNIT_TILES):
+                k3 = psum_k3.tile([P, H], F32)
+                product(k3, live["a", i], tiles[j], 1, True, True)
+                live["k3", i, j] = k3
 
-                rest = work.tile([P, UNIT_TILES, H], F32)
-                nc.vector.tensor_tensor(
-                    out=rest[:], in0=x_sb[s][:, here, :], in1=x_sb[s][:, after, :], op=SUBTRACT
+        def widen(i, name, row_tiles):
+            wide = lasting.tile([P, UNIT_TILES, PACK, P], F32, tag=name)
+            for j in range(UNIT_TILES):
+                nc.scalar.copy(
+                    out=wide[:, j, :, :].rearrange("p (u e) q -> p u e q", u=2),
+                    in_=by_word_value(row_tiles[j]),
                 )
-                nc.vector.scalar_tensor_tensor(
-                    out=rest[:], in0=k1_sb[s][:, here, :], scalar=1.0 / 6.0, in1=rest[:],
-                    op0=MULT, op1=ADD,
-                )
-                nc.vector.scalar_tensor_tensor(
-                    out=rest[:], in0=k2_sb[s][:, here, :], scalar=1.0 / 3.0, in1=rest[:],
-                    op0=MULT, op1=ADD,
-                )
+            live[name, i] = wide
 
-                half_k2 = work.tile([P, UNIT_TILES, H], BF16)
-                nc.scalar.activation(out=half_k2[:], in_=k2_sb[s][:, here, :], func=COPY, scale=0.5)
-                y_turned = transpose_pairs(
-                    nc, psum_pairs, identity, [x_sb[s][:, t0 + j, :] for j in range(UNIT_TILES)]
-                )
-                h_turned = transpose_pairs(
-                    nc, psum_pairs, identity, [half_k2[:, j, :] for j in range(UNIT_TILES)]
-                )
-                y_grouped = work.tile([P, UNIT_ROWS, PACK], BF16, align_bytes=64)
-                copy_pairs(nc, y_grouped, y_turned)
-                a_grouped = work.tile([P, UNIT_ROWS, PACK], BF16, align_bytes=64)
-                nc.vector.tensor_tensor(
-                    out=a_grouped[:].rearrange("p m (u e) -> p m u e", u=2),
-                    in0=h_turned[:].bitcast(BF16).rearrange("p u (m e) -> p m u e", e=2),
-                    in1=y_grouped[:].rearrange("p m (u e) -> p m u e", u=2),
-                    op=ADD,
-                )
-                a_codes = work.tile([P, UNIT_ROWS], U32, align_bytes=64)
-                a_scales = work.tile([P, UNIT_ROWS], U8, align_bytes=64)
-                quantise(nc, a_codes, a_scales, a_grouped)
+        def widen_y(i):
+            widen(i, "y_wide", [unit_rows(x_sb, i)[:, j, :] for j in range(UNIT_TILES)])
 
-                y_wide = work.tile([P, UNIT_TILES, PACK, P], F32)
-                k3_wide = work.tile([P, UNIT_TILES, PACK, P], F32)
-                b_grouped = work.tile([P, UNIT_ROWS, PACK], BF16, align_bytes=64)
-                for j in range(UNIT_TILES):
-                    nc.scalar.copy(
-                        out=y_wide[:, j, :, :].rearrange("p (u e) q -> p u e q", u=2),
-                        in_=by_word_value(x_sb[s][:, t0 + j, :]),
-                    )
-                    k3 = psum_k3.tile([P, H], F32)
-                    product(k3, (a_codes, a_scales), tiles[j], 1, True, True)
-                    nc.scalar.copy(
-                        out=k3_wide[:, j, :, :].rearrange("p (u e) q -> p u e q", u=2),
-                        in_=by_word_value(k3[:]),
-                    )
-                for j in range(UNIT_TILES):
-                    b_turned = psum_b.tile([P, PACK, P], F32)
-                    for t in range(PACK):
-                        for term, first in ((y_wide, True), (k3_wide, False)):
-                            nc.tensor.matmul(
-                                out=b_turned[:, t, :],
-                                lhsT=term[:, j, t, :],
-                                rhs=identity[:],
-                                start=first,
-                                stop=not first,
-                                is_transpose=True,
-                            )
-                    nc.scalar.copy(
-                        out=b_grouped[:, tiles[j], :], in_=b_turned[:].rearrange("p t n -> p n t")
-                    )
-                b_codes = work.tile([P, UNIT_ROWS], U32, align_bytes=64)
-                b_scales = work.tile([P, UNIT_ROWS], U8, align_bytes=64)
-                quantise(nc, b_codes, b_scales, b_grouped)
+        def widen_k3(i):
+            widen(i, "k3_wide", [live["k3", i, j][:] for j in range(UNIT_TILES)])
 
-                for j in range(UNIT_TILES):
-                    stages = psum_sum.tile([P, H], F32)
-                    product(stages, (a_codes, a_scales), tiles[j], 2, True, False)
-                    product(stages, (b_codes, b_scales), tiles[j], 1, False, True)
-                    nc.vector.scalar_tensor_tensor(
-                        out=rest[:, j, :], in0=stages[:], scalar=1.0 / 6.0, in1=rest[:, j, :],
-                        op0=MULT, op1=ADD,
-                    )
-                nc.sync.dma_start(out=out_rows[:, here, :], in_=rest[:])
+        def turn_b(i):
+            for j in range(UNIT_TILES):
+                b_turned = psum_b.tile([P, PACK, P], F32)
+                for t in range(PACK):
+                    for name, first in (("y_wide", True), ("k3_wide", False)):
+                        nc.tensor.matmul(
+                            out=b_turned[:, t, :],
+                            lhsT=live[name, i][:, j, t, :],
+                            rhs=identity[:],
+                            start=first,
+                            stop=not first,
+                            is_transpose=True,
+                        )
+                live["b_turned", i, j] = b_turned
+
+        def round_b(i):
+            b_grouped = work.tile([P, UNIT_ROWS, PACK], BF16, align_bytes=64)
+            for j in range(UNIT_TILES):
+                nc.scalar.copy(
+                    out=b_grouped[:, tiles[j], :],
+                    in_=live["b_turned", i, j][:].rearrange("p t n -> p n t"),
+                )
+            live["b_grouped", i] = b_grouped
+
+        def second_product(i):
+            for j in range(UNIT_TILES):
+                stages = psum_sum.tile([P, H], F32)
+                product(stages, live["a", i], tiles[j], 2, True, False)
+                product(stages, live["b", i], tiles[j], 1, False, True)
+                live["stages", i, j] = stages
+
+        def rest_difference(i):
+            s, t0 = units[i]
+            rest = lasting.tile([P, UNIT_TILES, H], F32)
+            nc.vector.tensor_tensor(
+                out=rest[:],
+                in0=x_sb[s][:, t0 : t0 + UNIT_TILES, :],
+                in1=x_sb[s][:, t0 + 1 : t0 + 1 + UNIT_TILES, :],
+                op=SUBTRACT,
+            )
+            live["rest", i] = rest
+
+        def rest_add(i, stage_sb, weight):
+            rest = live["rest", i]
+            nc.vector.scalar_tensor_tensor(
+                out=rest[:], in0=unit_rows(stage_sb, i), scalar=weight, in1=rest[:],
+                op0=MULT, op1=ADD,
+            )
+
+        def finish(i, j):
+            rest = live["rest", i]
+            nc.vector.scalar_tensor_tensor(
+                out=rest[:, j, :], in0=live["stages", i, j][:], scalar=1.0 / 6.0,
+                in1=rest[:, j, :], op0=MULT, op1=ADD,
+            )
+
+        def store(i):
+            s, t0 = units[i]
+            nc.sync.dma_start(
+                out=out[s].rearrange("(p t) h -> p t h", t=STATES_PER_PARTITION)[
+                    :, t0 : t0 + UNIT_TILES, :
+                ],
+                in_=live["rest", i][:],
+            )
+
+        def in_flight(i):
+            return 0 <= i < len(units)
+
+        def pipeline_round(r):
+            if in_flight(r - 2):
+                turn_b(r - 2)
+            if in_flight(r + 1):
+                halve_k2(r + 1)
+                widen_y(r + 1)
+            if in_flight(r - 3):
+                quantise_unit(r - 3, "b")
+                second_product(r - 3)
+            if in_flight(r):
+                rest_difference(r)
+            if in_flight(r - 1):
+                quantise_unit(r - 1, "a")
+                first_product(r - 1)
+            if in_flight(r):
+                rest_add(r, k1_sb, 1.0 / 6.0)
+                add_a(r)
+                turn_a(r)
+            if in_flight(r - 2):
+                round_b(r - 2)
+            if in_flight(r):
+                rest_add(r, k2_sb, 1.0 / 3.0)
+            if in_flight(r - 1):
+                widen_k3(r - 1)
+            if in_flight(r):
+                copy_a(r)
+            if in_flight(r - 3):
+                finish(r - 3, 0)
+                finish(r - 3, 1)
+                store(r - 3)
+
+        halve_k2(0)
+        widen_y(0)
+        turn_coefficients()
+        pipeline_round(0)
+        quantise_coefficients()
+        for r in range(1, len(units) + 3):
+            pipeline_round(r)

@@ -21,6 +21,9 @@ STEPS = 1024
 STATES_PER_PARTITION = STEPS // P
 UNIT_TILES = 2
 UNIT_ROWS = UNIT_TILES * P
+LOADS_AHEAD = 4
+STAGES_AFTER_A = 3
+REST_STEPS = 3
 
 FLOPS = 2 * 2 * SEQUENCES * STEPS * H * H
 
@@ -108,7 +111,7 @@ def tile_sindylossmixin_pa_t_kernel(tc, x, k1, k2, coefficients, out):
         load_unit(0)
         c_rows = consts.tile([P, PACK, H], BF16)
         nc.sync.dma_start(out=c_rows[:], in_=coefficients.rearrange("(i p) k -> p i k", p=P))
-        for i in range(1, len(units)):
+        for i in range(1, LOADS_AHEAD):
             load_unit(i)
 
         c_grouped = consts.tile([P, H, PACK], BF16, align_bytes=64)
@@ -248,6 +251,15 @@ def tile_sindylossmixin_pa_t_kernel(tc, x, k1, k2, coefficients, out):
                 op0=MULT, op1=ADD,
             )
 
+        def rest_step(k):
+            i, step = divmod(k, REST_STEPS)
+            if step == 0:
+                rest_difference(i)
+            elif step == 1:
+                rest_add(i, k1_sb, 1.0 / 6.0)
+            else:
+                rest_add(i, k2_sb, 1.0 / 3.0)
+
         def finish(i, j):
             rest = live["rest", i]
             nc.vector.scalar_tensor_tensor(
@@ -255,19 +267,28 @@ def tile_sindylossmixin_pa_t_kernel(tc, x, k1, k2, coefficients, out):
                 in1=rest[:, j, :], op0=MULT, op1=ADD,
             )
 
-        def store(i):
+        def store(i, j):
             s, t0 = units[i]
             nc.sync.dma_start(
-                out=out[s].rearrange("(p t) h -> p t h", t=STATES_PER_PARTITION)[
-                    :, t0 : t0 + UNIT_TILES, :
-                ],
-                in_=live["rest", i][:],
+                out=out[s].rearrange("(p t) h -> p t h", t=STATES_PER_PARTITION)[:, t0 + j, :],
+                in_=live["rest", i][:, j, :],
             )
 
         def in_flight(i):
             return 0 <= i < len(units)
 
+        rounds = len(units) + STAGES_AFTER_A
+        all_rest_steps = REST_STEPS * len(units)
+
         def pipeline_round(r):
+            rest_steps = list(
+                range(
+                    (r * all_rest_steps + rounds - 1) // rounds,
+                    ((r + 1) * all_rest_steps + rounds - 1) // rounds,
+                )
+            )
+            if in_flight(r + LOADS_AHEAD):
+                load_unit(r + LOADS_AHEAD)
             if in_flight(r - 2):
                 turn_b(r - 2)
             if in_flight(r + 1):
@@ -276,32 +297,31 @@ def tile_sindylossmixin_pa_t_kernel(tc, x, k1, k2, coefficients, out):
             if in_flight(r - 3):
                 quantise_unit(r - 3, "b")
                 second_product(r - 3)
-            if in_flight(r):
-                rest_difference(r)
+            rest_step(rest_steps[0])
             if in_flight(r - 1):
                 quantise_unit(r - 1, "a")
                 first_product(r - 1)
+            rest_step(rest_steps[1])
             if in_flight(r):
-                rest_add(r, k1_sb, 1.0 / 6.0)
                 add_a(r)
                 turn_a(r)
             if in_flight(r - 2):
                 round_b(r - 2)
-            if in_flight(r):
-                rest_add(r, k2_sb, 1.0 / 3.0)
+            for k in rest_steps[2:]:
+                rest_step(k)
             if in_flight(r - 1):
                 widen_k3(r - 1)
             if in_flight(r):
                 copy_a(r)
             if in_flight(r - 3):
-                finish(r - 3, 0)
-                finish(r - 3, 1)
-                store(r - 3)
+                for j in range(UNIT_TILES):
+                    finish(r - 3, j)
+                    store(r - 3, j)
 
         halve_k2(0)
         widen_y(0)
         turn_coefficients()
         pipeline_round(0)
         quantise_coefficients()
-        for r in range(1, len(units) + 3):
+        for r in range(1, rounds):
             pipeline_round(r)

@@ -24,12 +24,13 @@ UNIT_ROWS = UNIT_TILES * P
 LOADS_AHEAD = 4
 STAGES_AFTER_A = 3
 REST_STEPS = 3
+TENSOR_REST_UNITS = (1, 3, 5)
 
 FLOPS = 2 * 2 * SEQUENCES * STEPS * H * H
 
 
 def transpose_pairs(nc, psum_pairs, identity, row_tiles):
-    turned = psum_pairs.tile([P, 2, UNIT_ROWS], F32)
+    turned = psum_pairs.tile([P, 2, UNIT_ROWS], F32, tag="turned")
     for j, rows in enumerate(row_tiles):
         words = rows.bitcast(F32)
         for u in range(2):
@@ -72,6 +73,11 @@ def tile_sindylossmixin_pa_t_kernel(tc, x, k1, k2, coefficients, out):
 
         identity = consts.tile([P, P], F32)
         make_identity(nc, identity[:])
+        weighted = {}
+        for weight in (6.0, -6.0, 1.0, 2.0):
+            diagonal = consts.tile([P, P], BF16, tag="diagonal%d" % (weight + 6.0))
+            nc.vector.tensor_scalar_mul(out=diagonal[:], in0=identity[:], scalar1=weight)
+            weighted[weight] = diagonal
 
         x_sb, k1_sb, k2_sb = [], [], []
 
@@ -141,8 +147,11 @@ def tile_sindylossmixin_pa_t_kernel(tc, x, k1, k2, coefficients, out):
             return tiles_sb[s][:, t0 : t0 + UNIT_TILES, :]
 
         def halve_k2(i):
-            half_k2 = work.tile([P, UNIT_TILES, H], BF16)
-            nc.scalar.activation(out=half_k2[:], in_=unit_rows(k2_sb, i), func=COPY, scale=0.5)
+            half_k2 = work.tile([P, UNIT_TILES, H], BF16, tag="half_k2")
+            if i % 2 == 1:
+                nc.vector.tensor_scalar_mul(out=half_k2[:], in0=unit_rows(k2_sb, i), scalar1=0.5)
+            else:
+                nc.scalar.activation(out=half_k2[:], in_=unit_rows(k2_sb, i), func=COPY, scale=0.5)
             live["half_k2", i] = half_k2
 
         def add_a(i):
@@ -188,7 +197,7 @@ def tile_sindylossmixin_pa_t_kernel(tc, x, k1, k2, coefficients, out):
                 live["k3", i, j] = k3
 
         def widen(i, name, row_tiles):
-            wide = lasting.tile([P, UNIT_TILES, PACK, P], F32, tag=name)
+            wide = lasting.tile([P, UNIT_TILES, PACK, P], F32, tag=name, bufs=4)
             for j in range(UNIT_TILES):
                 nc.scalar.copy(
                     out=wide[:, j, :, :].rearrange("p (u e) q -> p u e q", u=2),
@@ -235,7 +244,7 @@ def tile_sindylossmixin_pa_t_kernel(tc, x, k1, k2, coefficients, out):
 
         def rest_difference(i):
             s, t0 = units[i]
-            rest = lasting.tile([P, UNIT_TILES, H], F32)
+            rest = lasting.tile([P, UNIT_TILES, H], F32, tag="rest", bufs=9)
             nc.vector.tensor_tensor(
                 out=rest[:],
                 in0=x_sb[s][:, t0 : t0 + UNIT_TILES, :],
@@ -251,8 +260,38 @@ def tile_sindylossmixin_pa_t_kernel(tc, x, k1, k2, coefficients, out):
                 op0=MULT, op1=ADD,
             )
 
+        def tensor_rest(i, j):
+            s, t0 = units[i]
+            t = t0 + j
+            terms = (
+                (6.0, x_sb[s][:, t, :]),
+                (-6.0, x_sb[s][:, t + 1, :]),
+                (2.0, k2_sb[s][:, t, :]),
+                (1.0, k1_sb[s][:, t, :]),
+            )
+            six_rest = psum_pairs.tile([P, H], F32, tag="turned")
+            for n, (weight, rows) in enumerate(terms):
+                nc.tensor.matmul(
+                    out=six_rest[:], lhsT=weighted[weight][:], rhs=rows,
+                    start=n == 0, stop=n == len(terms) - 1,
+                )
+            live["six_rest", i, j] = six_rest
+
+        def copy_tensor_rest(i, j):
+            if j == 0:
+                rest = lasting.tile([P, UNIT_TILES, H], F32, tag="rest", bufs=9)
+                live["rest", i] = rest
+            nc.scalar.activation(
+                out=live["rest", i][:, j, :], in_=live["six_rest", i, j][:], func=COPY,
+                scale=1.0 / 6.0,
+            )
+
+        vector_rest_units = [i for i in range(len(units)) if i not in TENSOR_REST_UNITS]
+        tensor_rest_tiles = [(i, j) for i in TENSOR_REST_UNITS for j in range(UNIT_TILES)]
+
         def rest_step(k):
-            i, step = divmod(k, REST_STEPS)
+            n, step = divmod(k, REST_STEPS)
+            i = vector_rest_units[n]
             if step == 0:
                 rest_difference(i)
             elif step == 1:
@@ -278,7 +317,7 @@ def tile_sindylossmixin_pa_t_kernel(tc, x, k1, k2, coefficients, out):
             return 0 <= i < len(units)
 
         rounds = len(units) + STAGES_AFTER_A
-        all_rest_steps = REST_STEPS * len(units)
+        all_rest_steps = REST_STEPS * len(vector_rest_units)
 
         def pipeline_round(r):
             rest_steps = list(
@@ -304,6 +343,8 @@ def tile_sindylossmixin_pa_t_kernel(tc, x, k1, k2, coefficients, out):
             rest_step(rest_steps[1])
             if in_flight(r):
                 add_a(r)
+                if r < len(tensor_rest_tiles):
+                    tensor_rest(*tensor_rest_tiles[r])
                 turn_a(r)
             if in_flight(r - 2):
                 round_b(r - 2)
@@ -311,6 +352,8 @@ def tile_sindylossmixin_pa_t_kernel(tc, x, k1, k2, coefficients, out):
                 rest_step(k)
             if in_flight(r - 1):
                 widen_k3(r - 1)
+            if r < len(tensor_rest_tiles):
+                copy_tensor_rest(*tensor_rest_tiles[r])
             if in_flight(r):
                 copy_a(r)
             if in_flight(r - 3):

@@ -146,9 +146,12 @@ def tile_sindylossmixin_pa_t_kernel(tc, x, k1, k2, coefficients, out):
             s, t0 = units[i]
             return tiles_sb[s][:, t0 : t0 + UNIT_TILES, :]
 
+        def halved_by_vector(i):
+            return i % 2 == 1
+
         def halve_k2(i):
             half_k2 = work.tile([P, UNIT_TILES, H], BF16, tag="half_k2")
-            if i % 2 == 1:
+            if halved_by_vector(i):
                 nc.vector.tensor_scalar_mul(out=half_k2[:], in0=unit_rows(k2_sb, i), scalar1=0.5)
             else:
                 nc.scalar.activation(out=half_k2[:], in_=unit_rows(k2_sb, i), func=COPY, scale=0.5)
@@ -211,20 +214,19 @@ def tile_sindylossmixin_pa_t_kernel(tc, x, k1, k2, coefficients, out):
         def widen_k3(i):
             widen(i, "k3_wide", [live["k3", i, j][:] for j in range(UNIT_TILES)])
 
-        def turn_b(i):
-            for j in range(UNIT_TILES):
-                b_turned = psum_b.tile([P, PACK, P], F32)
-                for t in range(PACK):
-                    for name, first in (("y_wide", True), ("k3_wide", False)):
-                        nc.tensor.matmul(
-                            out=b_turned[:, t, :],
-                            lhsT=live[name, i][:, j, t, :],
-                            rhs=identity[:],
-                            start=first,
-                            stop=not first,
-                            is_transpose=True,
-                        )
-                live["b_turned", i, j] = b_turned
+        def turn_b(i, j):
+            b_turned = psum_b.tile([P, PACK, P], F32)
+            for t in range(PACK):
+                for name, first in (("y_wide", True), ("k3_wide", False)):
+                    nc.tensor.matmul(
+                        out=b_turned[:, t, :],
+                        lhsT=live[name, i][:, j, t, :],
+                        rhs=identity[:],
+                        start=first,
+                        stop=not first,
+                        is_transpose=True,
+                    )
+            live["b_turned", i, j] = b_turned
 
         def round_b(i):
             b_grouped = work.tile([P, UNIT_ROWS, PACK], BF16, align_bytes=64)
@@ -329,13 +331,16 @@ def tile_sindylossmixin_pa_t_kernel(tc, x, k1, k2, coefficients, out):
             if in_flight(r + LOADS_AHEAD):
                 load_unit(r + LOADS_AHEAD)
             if in_flight(r - 2):
-                turn_b(r - 2)
+                turn_b(r - 2, 0)
             if in_flight(r + 1):
-                halve_k2(r + 1)
+                if not halved_by_vector(r + 1):
+                    halve_k2(r + 1)
                 widen_y(r + 1)
             if in_flight(r - 3):
                 quantise_unit(r - 3, "b")
                 second_product(r - 3)
+            if in_flight(r - 2):
+                turn_b(r - 2, 1)
             rest_step(rest_steps[0])
             if in_flight(r - 1):
                 quantise_unit(r - 1, "a")
@@ -360,6 +365,8 @@ def tile_sindylossmixin_pa_t_kernel(tc, x, k1, k2, coefficients, out):
                 for j in range(UNIT_TILES):
                     finish(r - 3, j)
                     store(r - 3, j)
+            if in_flight(r + 1) and halved_by_vector(r + 1):
+                halve_k2(r + 1)
 
         halve_k2(0)
         widen_y(0)

@@ -146,15 +146,9 @@ def tile_sindylossmixin_pa_t_kernel(tc, x, k1, k2, coefficients, out):
             s, t0 = units[i]
             return tiles_sb[s][:, t0 : t0 + UNIT_TILES, :]
 
-        def halved_by_vector(i):
-            return i % 2 == 1
-
         def halve_k2(i):
             half_k2 = work.tile([P, UNIT_TILES, H], BF16, tag="half_k2")
-            if halved_by_vector(i):
-                nc.vector.tensor_scalar_mul(out=half_k2[:], in0=unit_rows(k2_sb, i), scalar1=0.5)
-            else:
-                nc.scalar.activation(out=half_k2[:], in_=unit_rows(k2_sb, i), func=COPY, scale=0.5)
+            nc.vector.tensor_scalar_mul(out=half_k2[:], in0=unit_rows(k2_sb, i), scalar1=0.5)
             live["half_k2", i] = half_k2
 
         def add_a(i):
@@ -333,8 +327,6 @@ def tile_sindylossmixin_pa_t_kernel(tc, x, k1, k2, coefficients, out):
             if in_flight(r - 2):
                 turn_b(r - 2, 0)
             if in_flight(r + 1):
-                if not halved_by_vector(r + 1):
-                    halve_k2(r + 1)
                 widen_y(r + 1)
             if in_flight(r - 3):
                 quantise_unit(r - 3, "b")
@@ -365,7 +357,7 @@ def tile_sindylossmixin_pa_t_kernel(tc, x, k1, k2, coefficients, out):
                 for j in range(UNIT_TILES):
                     finish(r - 3, j)
                     store(r - 3, j)
-            if in_flight(r + 1) and halved_by_vector(r + 1):
+            if in_flight(r + 1):
                 halve_k2(r + 1)
 
         halve_k2(0)

@@ -24,6 +24,7 @@ UNIT_ROWS = UNIT_TILES * P
 LOADS_AHEAD = 4
 STAGES_AFTER_A = 3
 REST_STEPS = 3
+GPSIMD_COLUMNS = 384
 TENSOR_REST_UNITS = (1, 3, 5)
 
 FLOPS = 2 * 2 * SEQUENCES * STEPS * H * H
@@ -73,6 +74,7 @@ def tile_sindylossmixin_pa_t_kernel(tc, x, k1, k2, coefficients, out):
 
         identity = consts.tile([P, P], F32)
         make_identity(nc, identity[:])
+        started = consts.tile([P, 2], BF16)
         weighted = {}
         for weight in (6.0, -6.0, 1.0, 2.0):
             diagonal = consts.tile([P, P], BF16, tag="diagonal%d" % (weight + 6.0))
@@ -94,17 +96,18 @@ def tile_sindylossmixin_pa_t_kernel(tc, x, k1, k2, coefficients, out):
                 k2_sb.append(k2_tile)
                 k1_sb.append(k1_tile)
                 nc.sync.dma_start(
-                    out=x_tile[:, 0:1, :],
+                    out=x_tile[:, 0 : UNIT_TILES + 1, :],
                     in_=x[s, 0:STEPS, :].rearrange("(p t) h -> p t h", t=STATES_PER_PARTITION)[
-                        :, 0:1, :
+                        :, 0 : UNIT_TILES + 1, :
                     ],
                 )
-            nc.sync.dma_start(
-                out=x_sb[s][:, after, :],
-                in_=x[s, 1 : STEPS + 1, :].rearrange("(p t) h -> p t h", t=STATES_PER_PARTITION)[
-                    :, here, :
-                ],
-            )
+            else:
+                nc.sync.dma_start(
+                    out=x_sb[s][:, after, :],
+                    in_=x[s, 1 : STEPS + 1, :].rearrange(
+                        "(p t) h -> p t h", t=STATES_PER_PARTITION
+                    )[:, here, :],
+                )
             nc.sync.dma_start(
                 out=k2_sb[s][:, here, :],
                 in_=k2[rows, :].rearrange("(p t) h -> p t h", t=STATES_PER_PARTITION)[:, here, :],
@@ -132,13 +135,14 @@ def tile_sindylossmixin_pa_t_kernel(tc, x, k1, k2, coefficients, out):
                 )
                 copy_pairs(nc, c_grouped[:, half * UNIT_ROWS : (half + 1) * UNIT_ROWS, :], c_turned)
 
-        def quantise_coefficients():
+        def double_coefficients():
             nc.vector.tensor_scalar_mul(out=c_doubled[:], in0=c_grouped[:], scalar1=2.0)
-            for weight, grouped in ((1, c_grouped), (2, c_doubled)):
-                c_codes = consts.tile([P, H], U32, align_bytes=64, tag="c_codes%d" % weight)
-                c_scales = consts.tile([P, H], U8, align_bytes=64, tag="c_scales%d" % weight)
-                quantise(nc, c_codes, c_scales, grouped)
-                c_operand[weight] = (c_codes, c_scales)
+
+        def quantise_coefficients(weight):
+            c_codes = consts.tile([P, H], U32, align_bytes=64, tag="c_codes%d" % weight)
+            c_scales = consts.tile([P, H], U8, align_bytes=64, tag="c_scales%d" % weight)
+            quantise(nc, c_codes, c_scales, (None, c_grouped, c_doubled)[weight])
+            c_operand[weight] = (c_codes, c_scales)
 
         live = {}
 
@@ -239,15 +243,28 @@ def tile_sindylossmixin_pa_t_kernel(tc, x, k1, k2, coefficients, out):
                 live["stages", i, j] = stages
 
         def rest_difference(i):
+            done = GPSIMD_COLUMNS if ("rest", i) in live else 0
+            if done == 0:
+                rest = lasting.tile([P, UNIT_TILES, H], F32, tag="rest", bufs=9)
+                live["rest", i] = rest
+            difference(nc.vector, i, done, UNIT_TILES * H)
+
+        def difference(engine, i, first, end):
             s, t0 = units[i]
-            rest = lasting.tile([P, UNIT_TILES, H], F32, tag="rest", bufs=9)
-            nc.vector.tensor_tensor(
-                out=rest[:],
-                in0=x_sb[s][:, t0 : t0 + UNIT_TILES, :],
-                in1=x_sb[s][:, t0 + 1 : t0 + 1 + UNIT_TILES, :],
-                op=SUBTRACT,
+            flat = [
+                x_sb[s][:, t : t + UNIT_TILES, :].rearrange("p t h -> p (t h)")[:, first:end]
+                for t in (t0, t0 + 1)
+            ]
+            engine.tensor_tensor(
+                out=live["rest", i][:].rearrange("p t h -> p (t h)")[:, first:end],
+                in0=flat[0], in1=flat[1], op=SUBTRACT,
             )
+
+        def gpsimd_difference(i, after):
+            nc.gpsimd.tensor_copy(out=started[:], in_=after[:, 0, 0:2])
+            rest = lasting.tile([P, UNIT_TILES, H], F32, tag="rest", bufs=9)
             live["rest", i] = rest
+            difference(nc.gpsimd, i, 0, GPSIMD_COLUMNS)
 
         def rest_add(i, stage_sb, weight):
             rest = live["rest", i]
@@ -291,9 +308,9 @@ def tile_sindylossmixin_pa_t_kernel(tc, x, k1, k2, coefficients, out):
             if step == 0:
                 rest_difference(i)
             elif step == 1:
-                rest_add(i, k1_sb, 1.0 / 6.0)
-            else:
                 rest_add(i, k2_sb, 1.0 / 3.0)
+            else:
+                rest_add(i, k1_sb, 1.0 / 6.0)
 
         def finish(i, j):
             rest = live["rest", i]
@@ -334,10 +351,14 @@ def tile_sindylossmixin_pa_t_kernel(tc, x, k1, k2, coefficients, out):
             if in_flight(r - 2):
                 turn_b(r - 2, 1)
             rest_step(rest_steps[0])
+            if r == 0:
+                halve_k2(r)
             if in_flight(r - 1):
                 quantise_unit(r - 1, "a")
                 first_product(r - 1)
             rest_step(rest_steps[1])
+            for k in rest_steps[2:]:
+                rest_step(k)
             if in_flight(r):
                 add_a(r)
                 if r < len(tensor_rest_tiles):
@@ -345,8 +366,10 @@ def tile_sindylossmixin_pa_t_kernel(tc, x, k1, k2, coefficients, out):
                 turn_a(r)
             if in_flight(r - 2):
                 round_b(r - 2)
-            for k in rest_steps[2:]:
-                rest_step(k)
+            if in_flight(r + 1):
+                halve_k2(r + 1)
+                if in_flight(r - 3) and r < len(vector_rest_units):
+                    gpsimd_difference(vector_rest_units[r], live["a_rows", r])
             if in_flight(r - 1):
                 widen_k3(r - 1)
             if r < len(tensor_rest_tiles):
@@ -357,13 +380,14 @@ def tile_sindylossmixin_pa_t_kernel(tc, x, k1, k2, coefficients, out):
                 for j in range(UNIT_TILES):
                     finish(r - 3, j)
                     store(r - 3, j)
-            if in_flight(r + 1):
-                halve_k2(r + 1)
 
-        halve_k2(0)
         widen_y(0)
         turn_coefficients()
         pipeline_round(0)
-        quantise_coefficients()
-        for r in range(1, rounds):
+        quantise_coefficients(1)
+        pipeline_round(1)
+        double_coefficients()
+        pipeline_round(2)
+        quantise_coefficients(2)
+        for r in range(3, rounds):
             pipeline_round(r)

@@ -191,26 +191,23 @@ def tile_sindylossmixin_pa_t_kernel(tc, x, k1, k2, coefficients, out):
                 stop=stop,
             )
 
-        def first_product(i):
-            for j in range(UNIT_TILES):
-                k3 = psum_k3.tile([P, H], F32)
-                product(k3, live["a", i], tiles[j], 1, True, True)
-                live["k3", i, j] = k3
+        def first_product(i, j):
+            k3 = psum_k3.tile([P, H], F32)
+            product(k3, live["a", i], tiles[j], 1, True, True)
+            live["k3", i, j] = k3
 
-        def widen(i, name, row_tiles):
-            wide = lasting.tile([P, UNIT_TILES, PACK, P], F32, tag=name, bufs=4)
-            for j in range(UNIT_TILES):
-                nc.scalar.copy(
-                    out=wide[:, j, :, :].rearrange("p (u e) q -> p u e q", u=2),
-                    in_=by_word_value(row_tiles[j]),
-                )
-            live[name, i] = wide
+        def widen(i, j, name, rows):
+            wide = lasting.tile([P, PACK, P], F32, tag=name, bufs=8)
+            nc.scalar.copy(
+                out=wide[:].rearrange("p (u e) q -> p u e q", u=2), in_=by_word_value(rows)
+            )
+            live[name, i, j] = wide
 
-        def widen_y(i):
-            widen(i, "y_wide", [unit_rows(x_sb, i)[:, j, :] for j in range(UNIT_TILES)])
+        def widen_y(i, j):
+            widen(i, j, "y_wide", unit_rows(x_sb, i)[:, j, :])
 
-        def widen_k3(i):
-            widen(i, "k3_wide", [live["k3", i, j][:] for j in range(UNIT_TILES)])
+        def widen_k3(i, j):
+            widen(i, j, "k3_wide", live["k3", i, j][:])
 
         def turn_b(i, j):
             b_turned = psum_b.tile([P, PACK, P], F32)
@@ -218,7 +215,7 @@ def tile_sindylossmixin_pa_t_kernel(tc, x, k1, k2, coefficients, out):
                 for name, first in (("y_wide", True), ("k3_wide", False)):
                     nc.tensor.matmul(
                         out=b_turned[:, t, :],
-                        lhsT=live[name, i][:, j, t, :],
+                        lhsT=live[name, i, j][:, t, :],
                         rhs=identity[:],
                         start=first,
                         stop=not first,
@@ -226,21 +223,20 @@ def tile_sindylossmixin_pa_t_kernel(tc, x, k1, k2, coefficients, out):
                     )
             live["b_turned", i, j] = b_turned
 
-        def round_b(i):
-            b_grouped = work.tile([P, UNIT_ROWS, PACK], BF16, align_bytes=64)
-            for j in range(UNIT_TILES):
-                nc.scalar.copy(
-                    out=b_grouped[:, tiles[j], :],
-                    in_=live["b_turned", i, j][:].rearrange("p t n -> p n t"),
-                )
-            live["b_grouped", i] = b_grouped
+        def round_b(i, j):
+            if j == 0:
+                b_grouped = work.tile([P, UNIT_ROWS, PACK], BF16, align_bytes=64)
+                live["b_grouped", i] = b_grouped
+            nc.scalar.copy(
+                out=live["b_grouped", i][:, tiles[j], :],
+                in_=live["b_turned", i, j][:].rearrange("p t n -> p n t"),
+            )
 
-        def second_product(i):
-            for j in range(UNIT_TILES):
-                stages = psum_sum.tile([P, H], F32)
-                product(stages, live["a", i], tiles[j], 2, True, False)
-                product(stages, live["b", i], tiles[j], 1, False, True)
-                live["stages", i, j] = stages
+        def second_product(i, j):
+            stages = psum_sum.tile([P, H], F32)
+            product(stages, live["a", i], tiles[j], 2, True, False)
+            product(stages, live["b", i], tiles[j], 1, False, True)
+            live["stages", i, j] = stages
 
         def rest_difference(i):
             done = GPSIMD_COLUMNS if ("rest", i) in live else 0
@@ -261,7 +257,7 @@ def tile_sindylossmixin_pa_t_kernel(tc, x, k1, k2, coefficients, out):
             )
 
         def gpsimd_difference(i, after):
-            nc.gpsimd.tensor_copy(out=started[:], in_=after[:, 0, 0:2])
+            nc.gpsimd.tensor_copy(out=started[:], in_=after[:, UNIT_TILES - 1, H - 2 : H])
             rest = lasting.tile([P, UNIT_TILES, H], F32, tag="rest", bufs=9)
             live["rest", i] = rest
             difference(nc.gpsimd, i, 0, GPSIMD_COLUMNS)
@@ -341,47 +337,59 @@ def tile_sindylossmixin_pa_t_kernel(tc, x, k1, k2, coefficients, out):
             )
             if in_flight(r + LOADS_AHEAD):
                 load_unit(r + LOADS_AHEAD)
+            first, second = range(UNIT_TILES)
             if in_flight(r - 2):
-                turn_b(r - 2, 0)
+                turn_b(r - 2, first)
             if in_flight(r + 1):
-                widen_y(r + 1)
+                widen_y(r + 1, first)
+                widen_y(r + 1, second)
             if in_flight(r - 3):
                 quantise_unit(r - 3, "b")
-                second_product(r - 3)
-            if in_flight(r - 2):
-                turn_b(r - 2, 1)
-            rest_step(rest_steps[0])
+                second_product(r - 3, first)
             if r == 0:
+                rest_step(rest_steps[0])
                 halve_k2(r)
             if in_flight(r - 1):
                 quantise_unit(r - 1, "a")
-                first_product(r - 1)
-            rest_step(rest_steps[1])
-            for k in rest_steps[2:]:
-                rest_step(k)
+                first_product(r - 1, first)
+            if in_flight(r - 2):
+                turn_b(r - 2, second)
+                round_b(r - 2, first)
+            if r > 0:
+                rest_step(rest_steps[0])
             if in_flight(r):
                 add_a(r)
-                if r < len(tensor_rest_tiles):
-                    tensor_rest(*tensor_rest_tiles[r])
                 turn_a(r)
-            if in_flight(r - 2):
-                round_b(r - 2)
-            if in_flight(r + 1):
-                halve_k2(r + 1)
-                if in_flight(r - 3) and r < len(vector_rest_units):
-                    gpsimd_difference(vector_rest_units[r], live["a_rows", r])
             if in_flight(r - 1):
-                widen_k3(r - 1)
+                widen_k3(r - 1, first)
+            if in_flight(r - 2):
+                round_b(r - 2, second)
+            if in_flight(r - 3):
+                second_product(r - 3, second)
+            if in_flight(r - 1):
+                first_product(r - 1, second)
             if r < len(tensor_rest_tiles):
-                copy_tensor_rest(*tensor_rest_tiles[r])
+                tensor_rest(*tensor_rest_tiles[r])
+            for k in rest_steps[1:]:
+                rest_step(k)
             if in_flight(r):
                 copy_a(r)
+            if in_flight(r - 1):
+                widen_k3(r - 1, second)
+            if r < len(tensor_rest_tiles):
+                copy_tensor_rest(*tensor_rest_tiles[r])
+            if in_flight(r + 1):
+                if in_flight(r - 3) and r < len(vector_rest_units):
+                    last_rest = live["rest", vector_rest_units[rest_steps[-1] // REST_STEPS]]
+                    gpsimd_difference(vector_rest_units[r], last_rest)
+                halve_k2(r + 1)
             if in_flight(r - 3):
                 for j in range(UNIT_TILES):
                     finish(r - 3, j)
                     store(r - 3, j)
 
-        widen_y(0)
+        for j in range(UNIT_TILES):
+            widen_y(0, j)
         turn_coefficients()
         pipeline_round(0)
         quantise_coefficients(1)

@@ -24,25 +24,23 @@ UNIT_ROWS = UNIT_TILES * P
 LOADS_AHEAD = 4
 STAGES_AFTER_A = 3
 REST_STEPS = 3
-GPSIMD_COLUMNS = 384
+GPSIMD_COLUMNS = 320
 TENSOR_REST_UNITS = (1, 3, 5)
 
 FLOPS = 2 * 2 * SEQUENCES * STEPS * H * H
 
 
-def transpose_pairs(nc, psum_pairs, identity, row_tiles):
-    turned = psum_pairs.tile([P, 2, UNIT_ROWS], F32, tag="turned")
+def transpose_pairs(nc, turned, identity, row_tiles):
     for j, rows in enumerate(row_tiles):
         words = rows.bitcast(F32)
         for u in range(2):
             nc.tensor.transpose(
                 turned[:, u, j * P : (j + 1) * P], words[:, u * P : (u + 1) * P], identity[:]
             )
-    return turned
 
 
 def copy_pairs(nc, grouped, turned):
-    nc.scalar.copy(out=grouped[:].bitcast(F32), in_=turned[:].rearrange("p u m -> p m u"))
+    nc.scalar.copy(out=grouped.bitcast(F32), in_=turned[:].rearrange("p u m -> p m u"))
 
 
 def by_word_value(row):
@@ -51,7 +49,7 @@ def by_word_value(row):
 
 def quantise(nc, codes, scales, grouped):
     nc.vector.quantize_mx(
-        out=codes[:].bitcast(FP8X4), scales=scales[:], in_=grouped[:].rearrange("p m t -> p (m t)")
+        out=codes.bitcast(FP8X4), scales=scales, in_=grouped.rearrange("p m t -> p (m t)")
     )
 
 
@@ -66,10 +64,10 @@ def tile_sindylossmixin_pa_t_kernel(tc, x, k1, k2, coefficients, out):
         loads = ctx.enter_context(tc.tile_pool(name="loads", bufs=SEQUENCES))
         work = ctx.enter_context(tc.tile_pool(name="work", bufs=3))
         lasting = ctx.enter_context(tc.tile_pool(name="lasting", bufs=5))
-        psum_pairs = ctx.enter_context(tc.psum_pool(name="psum_pairs", bufs=2))
+        psum_a = ctx.enter_context(tc.psum_pool(name="psum_a", bufs=1))
         psum_b = ctx.enter_context(tc.psum_pool(name="psum_b", bufs=2))
         psum_k3 = ctx.enter_context(tc.psum_pool(name="psum_k3", bufs=2))
-        psum_sum = ctx.enter_context(tc.psum_pool(name="psum_sum", bufs=2))
+        psum_sum = ctx.enter_context(tc.psum_pool(name="psum_sum", bufs=3))
         ctx.enter_context(tc.manual_schedule())
 
         identity = consts.tile([P, P], F32)
@@ -129,8 +127,9 @@ def tile_sindylossmixin_pa_t_kernel(tc, x, k1, k2, coefficients, out):
 
         def turn_coefficients():
             for half in range(PACK // UNIT_TILES):
-                c_turned = transpose_pairs(
-                    nc, psum_pairs, identity,
+                c_turned = psum_k3.tile([P, 2, UNIT_ROWS], F32, tag="k3")
+                transpose_pairs(
+                    nc, c_turned, identity,
                     [c_rows[:, half * UNIT_TILES + j, :] for j in range(UNIT_TILES)],
                 )
                 copy_pairs(nc, c_grouped[:, half * UNIT_ROWS : (half + 1) * UNIT_ROWS, :], c_turned)
@@ -141,7 +140,7 @@ def tile_sindylossmixin_pa_t_kernel(tc, x, k1, k2, coefficients, out):
         def quantise_coefficients(weight):
             c_codes = consts.tile([P, H], U32, align_bytes=64, tag="c_codes%d" % weight)
             c_scales = consts.tile([P, H], U8, align_bytes=64, tag="c_scales%d" % weight)
-            quantise(nc, c_codes, c_scales, (None, c_grouped, c_doubled)[weight])
+            quantise(nc, c_codes[:], c_scales[:], (None, c_grouped, c_doubled)[weight][:])
             c_operand[weight] = (c_codes, c_scales)
 
         live = {}
@@ -163,23 +162,39 @@ def tile_sindylossmixin_pa_t_kernel(tc, x, k1, k2, coefficients, out):
             live["a_rows", i] = a_rows
 
         def turn_a(i):
-            live["a_turned", i] = transpose_pairs(
-                nc, psum_pairs, identity, [live["a_rows", i][:, j, :] for j in range(UNIT_TILES)]
+            a_turned = psum_a.tile([P, 2, UNIT_ROWS], F32)
+            transpose_pairs(
+                nc, a_turned, identity, [live["a_rows", i][:, j, :] for j in range(UNIT_TILES)]
             )
+            live["a_turned", i] = a_turned
+
+        def open_grouped(r):
+            grouped = work.tile([P, 2 * UNIT_ROWS, PACK], BF16, align_bytes=64)
+            live["grouped", r] = grouped
+
+        def b_rows_grouped(i):
+            return live["grouped", i + 3][:, :UNIT_ROWS, :]
+
+        def a_rows_grouped(i):
+            return live["grouped", i + 1][:, UNIT_ROWS:, :]
 
         def copy_a(i):
-            a_grouped = work.tile([P, UNIT_ROWS, PACK], BF16, align_bytes=64)
-            copy_pairs(nc, a_grouped, live["a_turned", i])
-            live["a_grouped", i] = a_grouped
+            copy_pairs(nc, a_rows_grouped(i), live["a_turned", i])
 
-        def quantise_unit(i, operand):
-            codes = lasting.tile([P, UNIT_ROWS], U32, align_bytes=64, tag=operand + "_codes")
-            scales = lasting.tile([P, UNIT_ROWS], U8, align_bytes=64, tag=operand + "_scales")
-            quantise(nc, codes, scales, live[operand + "_grouped", i])
-            live[operand, i] = (codes, scales)
+        def quantise_round(r):
+            first = 0 if in_flight(r - 3) else UNIT_ROWS
+            end = 2 * UNIT_ROWS if in_flight(r - 1) else UNIT_ROWS
+            codes = lasting.tile([P, 2 * UNIT_ROWS], U32, align_bytes=64)
+            scales = lasting.tile([P, 2 * UNIT_ROWS], U8, align_bytes=64)
+            quantise(
+                nc, codes[:, first:end], scales[:, first:end], live["grouped", r][:, first:end, :]
+            )
+            live["b", r - 3] = (codes, scales, 0)
+            live["a", r - 1] = (codes, scales, UNIT_ROWS)
 
-        def product(acc, rows_operand, tile_rows, weight, start, stop):
-            codes, scales = rows_operand
+        def product(acc, rows_operand, j, weight, start, stop):
+            codes, scales, first_row = rows_operand
+            tile_rows = slice(first_row + j * P, first_row + (j + 1) * P)
             c_codes, c_scales = c_operand[weight]
             nc.tensor.matmul_mx(
                 out=acc[:],
@@ -192,8 +207,8 @@ def tile_sindylossmixin_pa_t_kernel(tc, x, k1, k2, coefficients, out):
             )
 
         def first_product(i, j):
-            k3 = psum_k3.tile([P, H], F32)
-            product(k3, live["a", i], tiles[j], 1, True, True)
+            k3 = psum_k3.tile([P, H], F32, tag="k3")
+            product(k3, live["a", i], j, 1, True, True)
             live["k3", i, j] = k3
 
         def widen(i, j, name, rows):
@@ -224,26 +239,27 @@ def tile_sindylossmixin_pa_t_kernel(tc, x, k1, k2, coefficients, out):
             live["b_turned", i, j] = b_turned
 
         def round_b(i, j):
-            if j == 0:
-                b_grouped = work.tile([P, UNIT_ROWS, PACK], BF16, align_bytes=64)
-                live["b_grouped", i] = b_grouped
             nc.scalar.copy(
-                out=live["b_grouped", i][:, tiles[j], :],
+                out=b_rows_grouped(i)[:, tiles[j], :],
                 in_=live["b_turned", i, j][:].rearrange("p t n -> p n t"),
             )
 
         def second_product(i, j):
-            stages = psum_sum.tile([P, H], F32)
-            product(stages, live["a", i], tiles[j], 2, True, False)
-            product(stages, live["b", i], tiles[j], 1, False, True)
+            stages = psum_sum.tile([P, H], F32, tag="sum")
+            product(stages, live["a", i], j, 2, True, False)
+            product(stages, live["b", i], j, 1, False, True)
             live["stages", i, j] = stages
 
         def rest_difference(i):
-            done = GPSIMD_COLUMNS if ("rest", i) in live else 0
-            if done == 0:
+            open_rest(i)
+            difference(nc.vector, i, gpsimd_columns.get(i, 0), UNIT_TILES * H)
+
+        gpsimd_columns = {}
+
+        def open_rest(i):
+            if ("rest", i) not in live:
                 rest = lasting.tile([P, UNIT_TILES, H], F32, tag="rest", bufs=9)
                 live["rest", i] = rest
-            difference(nc.vector, i, done, UNIT_TILES * H)
 
         def difference(engine, i, first, end):
             s, t0 = units[i]
@@ -258,9 +274,10 @@ def tile_sindylossmixin_pa_t_kernel(tc, x, k1, k2, coefficients, out):
 
         def gpsimd_difference(i, after):
             nc.gpsimd.tensor_copy(out=started[:], in_=after[:, UNIT_TILES - 1, H - 2 : H])
-            rest = lasting.tile([P, UNIT_TILES, H], F32, tag="rest", bufs=9)
-            live["rest", i] = rest
-            difference(nc.gpsimd, i, 0, GPSIMD_COLUMNS)
+            open_rest(i)
+            first = gpsimd_columns.get(i, 0)
+            gpsimd_columns[i] = first + GPSIMD_COLUMNS
+            difference(nc.gpsimd, i, first, first + GPSIMD_COLUMNS)
 
         def rest_add(i, stage_sb, weight):
             rest = live["rest", i]
@@ -278,7 +295,7 @@ def tile_sindylossmixin_pa_t_kernel(tc, x, k1, k2, coefficients, out):
                 (2.0, k2_sb[s][:, t, :]),
                 (1.0, k1_sb[s][:, t, :]),
             )
-            six_rest = psum_pairs.tile([P, H], F32, tag="turned")
+            six_rest = psum_sum.tile([P, H], F32, tag="sum")
             for n, (weight, rows) in enumerate(terms):
                 nc.tensor.matmul(
                     out=six_rest[:], lhsT=weighted[weight][:], rhs=rows,
@@ -328,38 +345,41 @@ def tile_sindylossmixin_pa_t_kernel(tc, x, k1, k2, coefficients, out):
         rounds = len(units) + STAGES_AFTER_A
         all_rest_steps = REST_STEPS * len(vector_rest_units)
 
-        def pipeline_round(r):
-            rest_steps = list(
+        def rest_steps_of(r):
+            return list(
                 range(
                     (r * all_rest_steps + rounds - 1) // rounds,
                     ((r + 1) * all_rest_steps + rounds - 1) // rounds,
                 )
             )
+
+        def pipeline_round(r):
+            rest_steps = rest_steps_of(r)
+            if r == 0:
+                rest_steps = rest_steps[2:]
             if in_flight(r + LOADS_AHEAD):
                 load_unit(r + LOADS_AHEAD)
             first, second = range(UNIT_TILES)
             if in_flight(r - 2):
                 turn_b(r - 2, first)
-            if in_flight(r + 1):
-                widen_y(r + 1, first)
-                widen_y(r + 1, second)
+            if in_flight(r):
+                turn_a(r)
+            if in_flight(r - 3) or in_flight(r - 1):
+                quantise_round(r)
             if in_flight(r - 3):
-                quantise_unit(r - 3, "b")
                 second_product(r - 3, first)
-            if r == 0:
-                rest_step(rest_steps[0])
-                halve_k2(r)
             if in_flight(r - 1):
-                quantise_unit(r - 1, "a")
                 first_product(r - 1, first)
+            if in_flight(r - 2) or in_flight(r):
+                open_grouped(r + 1)
             if in_flight(r - 2):
                 turn_b(r - 2, second)
                 round_b(r - 2, first)
-            if r > 0:
-                rest_step(rest_steps[0])
             if in_flight(r):
-                add_a(r)
-                turn_a(r)
+                copy_a(r)
+            rest_step(rest_steps[0])
+            if in_flight(r + 1):
+                halve_k2(r + 1)
             if in_flight(r - 1):
                 widen_k3(r - 1, first)
             if in_flight(r - 2):
@@ -372,24 +392,31 @@ def tile_sindylossmixin_pa_t_kernel(tc, x, k1, k2, coefficients, out):
                 tensor_rest(*tensor_rest_tiles[r])
             for k in rest_steps[1:]:
                 rest_step(k)
-            if in_flight(r):
-                copy_a(r)
             if in_flight(r - 1):
                 widen_k3(r - 1, second)
+            if in_flight(r + 1):
+                widen_y(r + 1, first)
+            if in_flight(r + 1):
+                widen_y(r + 1, second)
             if r < len(tensor_rest_tiles):
                 copy_tensor_rest(*tensor_rest_tiles[r])
+            if in_flight(r - 3) and r < len(units):
+                n = r if r < len(vector_rest_units) else r - 3
+                last_rest = live["rest", vector_rest_units[rest_steps[-1] // REST_STEPS]]
+                gpsimd_difference(vector_rest_units[n], last_rest)
             if in_flight(r + 1):
-                if in_flight(r - 3) and r < len(vector_rest_units):
-                    last_rest = live["rest", vector_rest_units[rest_steps[-1] // REST_STEPS]]
-                    gpsimd_difference(vector_rest_units[r], last_rest)
-                halve_k2(r + 1)
-            if in_flight(r - 3):
-                for j in range(UNIT_TILES):
-                    finish(r - 3, j)
-                    store(r - 3, j)
+                add_a(r + 1)
+            for i, j in ((r - 3, first), (r - 4, second)):
+                if in_flight(i):
+                    finish(i, j)
+                    store(i, j)
 
         for j in range(UNIT_TILES):
             widen_y(0, j)
+        rest_step(rest_steps_of(0)[0])
+        halve_k2(0)
+        rest_step(rest_steps_of(0)[1])
+        add_a(0)
         turn_coefficients()
         pipeline_round(0)
         quantise_coefficients(1)
@@ -399,3 +426,5 @@ def tile_sindylossmixin_pa_t_kernel(tc, x, k1, k2, coefficients, out):
         quantise_coefficients(2)
         for r in range(3, rounds):
             pipeline_round(r)
+        finish(len(units) - 1, UNIT_TILES - 1)
+        store(len(units) - 1, UNIT_TILES - 1)

@@ -25,7 +25,9 @@ LOADS_AHEAD = 4
 STAGES_AFTER_A = 3
 REST_STEPS = 3
 GPSIMD_COLUMNS = 320
-TENSOR_REST_UNITS = (1, 3, 5)
+TENSOR_REST_UNITS = (1, 5, 9)
+TENSOR_COLUMNS_UNIT = 13
+TENSOR_COLUMNS = 192
 
 FLOPS = 2 * 2 * SEQUENCES * STEPS * H * H
 
@@ -150,8 +152,23 @@ def tile_sindylossmixin_pa_t_kernel(tc, x, k1, k2, coefficients, out):
             return tiles_sb[s][:, t0 : t0 + UNIT_TILES, :]
 
         def halve_k2(i):
-            half_k2 = work.tile([P, UNIT_TILES, H], BF16, tag="half_k2")
+            if shared(i):
+                nc.vector.tensor_scalar_mul(
+                    out=live["half_k2", i][:, 1, :], in0=unit_rows(k2_sb, i)[:, 1, :], scalar1=0.5
+                )
+                return
+            half_k2 = work.tile([P, UNIT_TILES, H], BF16, tag="half_k2", bufs=4)
             nc.vector.tensor_scalar_mul(out=half_k2[:], in0=unit_rows(k2_sb, i), scalar1=0.5)
+            live["half_k2", i] = half_k2
+
+        def shared(i):
+            return i % 2 == 0 and i > 3
+
+        def scalar_halve(i):
+            half_k2 = work.tile([P, UNIT_TILES, H], BF16, tag="half_k2", bufs=4)
+            nc.scalar.activation(
+                out=half_k2[:, 0, :], in_=unit_rows(k2_sb, i)[:, 0, :], func=COPY, scale=0.5
+            )
             live["half_k2", i] = half_k2
 
         def add_a(i):
@@ -252,9 +269,9 @@ def tile_sindylossmixin_pa_t_kernel(tc, x, k1, k2, coefficients, out):
 
         def rest_difference(i):
             open_rest(i)
-            difference(nc.vector, i, gpsimd_columns.get(i, 0), UNIT_TILES * H)
+            difference(nc.vector, i, taken.get(i, 0), UNIT_TILES * H)
 
-        gpsimd_columns = {}
+        taken = {TENSOR_COLUMNS_UNIT: TENSOR_COLUMNS}
 
         def open_rest(i):
             if ("rest", i) not in live:
@@ -275,18 +292,19 @@ def tile_sindylossmixin_pa_t_kernel(tc, x, k1, k2, coefficients, out):
         def gpsimd_difference(i, after):
             nc.gpsimd.tensor_copy(out=started[:], in_=after[:, UNIT_TILES - 1, H - 2 : H])
             open_rest(i)
-            first = gpsimd_columns.get(i, 0)
-            gpsimd_columns[i] = first + GPSIMD_COLUMNS
+            first = taken.get(i, 0)
+            taken[i] = first + GPSIMD_COLUMNS
             difference(nc.gpsimd, i, first, first + GPSIMD_COLUMNS)
 
         def rest_add(i, stage_sb, weight):
-            rest = live["rest", i]
+            first = TENSOR_COLUMNS if i == TENSOR_COLUMNS_UNIT else 0
+            rest = live["rest", i][:].rearrange("p t h -> p (t h)")[:, first:]
+            rows = unit_rows(stage_sb, i).rearrange("p t h -> p (t h)")[:, first:]
             nc.vector.scalar_tensor_tensor(
-                out=rest[:], in0=unit_rows(stage_sb, i), scalar=weight, in1=rest[:],
-                op0=MULT, op1=ADD,
+                out=rest, in0=rows, scalar=weight, in1=rest, op0=MULT, op1=ADD
             )
 
-        def tensor_rest(i, j):
+        def tensor_rest(i, j, columns=slice(0, H)):
             s, t0 = units[i]
             t = t0 + j
             terms = (
@@ -298,18 +316,16 @@ def tile_sindylossmixin_pa_t_kernel(tc, x, k1, k2, coefficients, out):
             six_rest = psum_sum.tile([P, H], F32, tag="sum")
             for n, (weight, rows) in enumerate(terms):
                 nc.tensor.matmul(
-                    out=six_rest[:], lhsT=weighted[weight][:], rhs=rows,
+                    out=six_rest[:, columns], lhsT=weighted[weight][:], rhs=rows[:, columns],
                     start=n == 0, stop=n == len(terms) - 1,
                 )
             live["six_rest", i, j] = six_rest
 
-        def copy_tensor_rest(i, j):
-            if j == 0:
-                rest = lasting.tile([P, UNIT_TILES, H], F32, tag="rest", bufs=9)
-                live["rest", i] = rest
+        def copy_tensor_rest(i, j, columns=slice(0, H)):
+            open_rest(i)
             nc.scalar.activation(
-                out=live["rest", i][:, j, :], in_=live["six_rest", i, j][:], func=COPY,
-                scale=1.0 / 6.0,
+                out=live["rest", i][:, j, columns], in_=live["six_rest", i, j][:, columns],
+                func=COPY, scale=1.0 / 6.0,
             )
 
         vector_rest_units = [i for i in range(len(units)) if i not in TENSOR_REST_UNITS]
@@ -382,14 +398,18 @@ def tile_sindylossmixin_pa_t_kernel(tc, x, k1, k2, coefficients, out):
                 halve_k2(r + 1)
             if in_flight(r - 1):
                 widen_k3(r - 1, first)
+            if in_flight(r + 2) and shared(r + 2):
+                scalar_halve(r + 2)
             if in_flight(r - 2):
                 round_b(r - 2, second)
             if in_flight(r - 3):
                 second_product(r - 3, second)
             if in_flight(r - 1):
                 first_product(r - 1, second)
-            if r < len(tensor_rest_tiles):
-                tensor_rest(*tensor_rest_tiles[r])
+            if 0 <= r - 1 < 2 * len(tensor_rest_tiles) and (r - 1) % 2 == 0:
+                tensor_rest(*tensor_rest_tiles[(r - 1) // 2])
+            if r == TENSOR_COLUMNS_UNIT:
+                tensor_rest(r, 0, slice(0, TENSOR_COLUMNS))
             for k in rest_steps[1:]:
                 rest_step(k)
             if in_flight(r - 1):
@@ -398,9 +418,11 @@ def tile_sindylossmixin_pa_t_kernel(tc, x, k1, k2, coefficients, out):
                 widen_y(r + 1, first)
             if in_flight(r + 1):
                 widen_y(r + 1, second)
-            if r < len(tensor_rest_tiles):
-                copy_tensor_rest(*tensor_rest_tiles[r])
-            if in_flight(r - 3) and r < len(units):
+            if 0 <= r - 1 < 2 * len(tensor_rest_tiles) and (r - 1) % 2 == 0:
+                copy_tensor_rest(*tensor_rest_tiles[(r - 1) // 2])
+            if r == TENSOR_COLUMNS_UNIT:
+                copy_tensor_rest(r, 0, slice(0, TENSOR_COLUMNS))
+            if in_flight(r - 4) and r < len(units):
                 n = r if r < len(vector_rest_units) else r - 3
                 last_rest = live["rest", vector_rest_units[rest_steps[-1] // REST_STEPS]]
                 gpsimd_difference(vector_rest_units[n], last_rest)

@@ -95,12 +95,13 @@ def tile_sindylossmixin_pa_t_kernel(tc, x, k1, k2, coefficients, out):
                 x_sb.append(x_tile)
                 k2_sb.append(k2_tile)
                 k1_sb.append(k1_tile)
-                nc.sync.dma_start(
-                    out=x_tile[:, 0 : UNIT_TILES + 1, :],
-                    in_=x[s, 0:STEPS, :].rearrange("(p t) h -> p t h", t=STATES_PER_PARTITION)[
-                        :, 0 : UNIT_TILES + 1, :
-                    ],
-                )
+                for part in (slice(0, UNIT_TILES), slice(UNIT_TILES, UNIT_TILES + 1)):
+                    nc.sync.dma_start(
+                        out=x_tile[:, part, :],
+                        in_=x[s, 0:STEPS, :].rearrange(
+                            "(p t) h -> p t h", t=STATES_PER_PARTITION
+                        )[:, part, :],
+                    )
             else:
                 nc.sync.dma_start(
                     out=x_sb[s][:, after, :],
@@ -269,7 +270,11 @@ def tile_sindylossmixin_pa_t_kernel(tc, x, k1, k2, coefficients, out):
 
         def rest_difference(i):
             open_rest(i)
-            difference(nc.vector, i, taken.get(i, 0), UNIT_TILES * H)
+            if i == 0:
+                difference(nc.vector, i, 0, H)
+                difference(nc.vector, i, H, UNIT_TILES * H)
+            else:
+                difference(nc.vector, i, taken.get(i, 0), UNIT_TILES * H)
 
         taken = {TENSOR_COLUMNS_UNIT: TENSOR_COLUMNS}
 
@@ -313,7 +318,7 @@ def tile_sindylossmixin_pa_t_kernel(tc, x, k1, k2, coefficients, out):
                 (2.0, k2_sb[s][:, t, :]),
                 (1.0, k1_sb[s][:, t, :]),
             )
-            six_rest = psum_sum.tile([P, H], F32, tag="sum")
+            six_rest = psum_k3.tile([P, H], F32, tag="k3")
             for n, (weight, rows) in enumerate(terms):
                 nc.tensor.matmul(
                     out=six_rest[:, columns], lhsT=weighted[weight][:], rhs=rows[:, columns],
@@ -341,18 +346,18 @@ def tile_sindylossmixin_pa_t_kernel(tc, x, k1, k2, coefficients, out):
             else:
                 rest_add(i, k1_sb, 1.0 / 6.0)
 
-        def finish(i, j):
+        def finish(i, j, columns=slice(0, H)):
             rest = live["rest", i]
             nc.vector.scalar_tensor_tensor(
-                out=rest[:, j, :], in0=live["stages", i, j][:], scalar=1.0 / 6.0,
-                in1=rest[:, j, :], op0=MULT, op1=ADD,
+                out=rest[:, j, columns], in0=live["stages", i, j][:, columns], scalar=1.0 / 6.0,
+                in1=rest[:, j, columns], op0=MULT, op1=ADD,
             )
 
-        def store(i, j):
+        def store(i, j, columns=slice(0, H)):
             s, t0 = units[i]
             nc.sync.dma_start(
-                out=out[s].rearrange("(p t) h -> p t h", t=STATES_PER_PARTITION)[:, t0 + j, :],
-                in_=live["rest", i][:, j, :],
+                out=out[s].rearrange("(p t) h -> p t h", t=STATES_PER_PARTITION)[:, t0 + j, columns],
+                in_=live["rest", i][:, j, columns],
             )
 
         def in_flight(i):
@@ -368,6 +373,10 @@ def tile_sindylossmixin_pa_t_kernel(tc, x, k1, k2, coefficients, out):
                     ((r + 1) * all_rest_steps + rounds - 1) // rounds,
                 )
             )
+
+        def finish_and_store(i, j, columns=slice(0, H)):
+            finish(i, j, columns)
+            store(i, j, columns)
 
         def pipeline_round(r):
             rest_steps = rest_steps_of(r)
@@ -394,6 +403,8 @@ def tile_sindylossmixin_pa_t_kernel(tc, x, k1, k2, coefficients, out):
             if in_flight(r):
                 copy_a(r)
             rest_step(rest_steps[0])
+            if r >= len(units):
+                finish_and_store(r - 4, second)
             if in_flight(r + 1):
                 halve_k2(r + 1)
             if in_flight(r - 1):
@@ -428,10 +439,10 @@ def tile_sindylossmixin_pa_t_kernel(tc, x, k1, k2, coefficients, out):
                 gpsimd_difference(vector_rest_units[n], last_rest)
             if in_flight(r + 1):
                 add_a(r + 1)
-            for i, j in ((r - 3, first), (r - 4, second)):
-                if in_flight(i):
-                    finish(i, j)
-                    store(i, j)
+            if in_flight(r - 3):
+                finish_and_store(r - 3, first)
+            if in_flight(r - 4) and r < len(units):
+                finish_and_store(r - 4, second)
 
         for j in range(UNIT_TILES):
             widen_y(0, j)
@@ -448,5 +459,6 @@ def tile_sindylossmixin_pa_t_kernel(tc, x, k1, k2, coefficients, out):
         quantise_coefficients(2)
         for r in range(3, rounds):
             pipeline_round(r)
-        finish(len(units) - 1, UNIT_TILES - 1)
-        store(len(units) - 1, UNIT_TILES - 1)
+        for half in range(2):
+            columns = slice(half * H // 2, (half + 1) * H // 2)
+            finish_and_store(len(units) - 1, UNIT_TILES - 1, columns)

from contextlib import ExitStack

import concourse.mybir as mybir
from concourse.masks import make_identity

F32 = mybir.dt.float32
BF16 = mybir.dt.bfloat16
U32 = mybir.dt.uint32
U8 = mybir.dt.uint8
FP8X4 = mybir.dt.float8_e4m3fn_x4
ADD = mybir.AluOpType.add
SUBTRACT = mybir.AluOpType.subtract
MULT = mybir.AluOpType.mult
COPY = mybir.ActivationFunctionType.Copy

P = 128
H = 512
PACK = 4
SEQUENCES = 4
STEPS = 1024
STATES_PER_PARTITION = STEPS // P
UNIT_TILES = 2
UNIT_ROWS = UNIT_TILES * P
LOADS_AHEAD = 4
STAGES_AFTER_A = 3
REST_STEPS = 3
GPSIMD_COLUMNS = 320
TENSOR_REST_UNITS = (1, 5, 9)
TENSOR_COLUMNS_UNIT = 13
TENSOR_COLUMNS = 192

FLOPS = 2 * 2 * SEQUENCES * STEPS * H * H


def transpose_pairs(nc, turned, identity, row_tiles):
    for j, rows in enumerate(row_tiles):
        words = rows.bitcast(F32)
        for u in range(2):
            nc.tensor.transpose(
                turned[:, u, j * P : (j + 1) * P], words[:, u * P : (u + 1) * P], identity[:]
            )


def copy_pairs(nc, grouped, turned):
    nc.scalar.copy(out=grouped.bitcast(F32), in_=turned[:].rearrange("p u m -> p m u"))


def by_word_value(row):
    return row.rearrange("p (u q e) -> p u e q", u=2, e=2)


def quantise(nc, codes, scales, grouped):
    nc.vector.quantize_mx(
        out=codes.bitcast(FP8X4), scales=scales, in_=grouped.rearrange("p m t -> p (m t)")
    )


def tile_sindylossmixin_pa_t_kernel(tc, x, k1, k2, coefficients, out):
    nc = tc.nc
    units = [
        (s, t0) for s in range(SEQUENCES) for t0 in range(0, STATES_PER_PARTITION, UNIT_TILES)
    ]
    tiles = [slice(j * P, (j + 1) * P) for j in range(UNIT_TILES)]
    with ExitStack() as ctx:
        consts = ctx.enter_context(tc.tile_pool(name="consts", bufs=1))
        loads = ctx.enter_context(tc.tile_pool(name="loads", bufs=SEQUENCES))
        work = ctx.enter_context(tc.tile_pool(name="work", bufs=3))
        lasting = ctx.enter_context(tc.tile_pool(name="lasting", bufs=5))
        psum_a = ctx.enter_context(tc.psum_pool(name="psum_a", bufs=1))
        psum_b = ctx.enter_context(tc.psum_pool(name="psum_b", bufs=2))
        psum_k3 = ctx.enter_context(tc.psum_pool(name="psum_k3", bufs=2))
        psum_sum = ctx.enter_context(tc.psum_pool(name="psum_sum", bufs=3))
        ctx.enter_context(tc.manual_schedule())

        identity = consts.tile([P, P], F32)
        make_identity(nc, identity[:])
        started = consts.tile([P, 2], BF16)
        weighted = {}
        for weight in (6.0, -6.0, 1.0, 2.0):
            diagonal = consts.tile([P, P], BF16, tag="diagonal%d" % (weight + 6.0))
            nc.vector.tensor_scalar_mul(out=diagonal[:], in0=identity[:], scalar1=weight)
            weighted[weight] = diagonal

        x_sb, k1_sb, k2_sb = [], [], []

        def load_unit(i):
            s, t0 = units[i]
            here = slice(t0, t0 + UNIT_TILES)
            after = slice(t0 + 1, t0 + 1 + UNIT_TILES)
            rows = slice(s * STEPS, (s + 1) * STEPS)
            if t0 == 0:
                x_tile = loads.tile([P, STATES_PER_PARTITION + 1, H], BF16)
                k2_tile = loads.tile([P, STATES_PER_PARTITION, H], BF16)
                k1_tile = loads.tile([P, STATES_PER_PARTITION, H], BF16)
                x_sb.append(x_tile)
                k2_sb.append(k2_tile)
                k1_sb.append(k1_tile)
                for part in (slice(0, UNIT_TILES), slice(UNIT_TILES, UNIT_TILES + 1)):
                    nc.sync.dma_start(
                        out=x_tile[:, part, :],
                        in_=x[s, 0:STEPS, :].rearrange(
                            "(p t) h -> p t h", t=STATES_PER_PARTITION
                        )[:, part, :],
                    )
            else:
                nc.sync.dma_start(
                    out=x_sb[s][:, after, :],
                    in_=x[s, 1 : STEPS + 1, :].rearrange(
                        "(p t) h -> p t h", t=STATES_PER_PARTITION
                    )[:, here, :],
                )
            nc.sync.dma_start(
                out=k2_sb[s][:, here, :],
                in_=k2[rows, :].rearrange("(p t) h -> p t h", t=STATES_PER_PARTITION)[:, here, :],
            )
            nc.sync.dma_start(
                out=k1_sb[s][:, here, :],
                in_=k1[rows, :].rearrange("(p t) h -> p t h", t=STATES_PER_PARTITION)[:, here, :],
            )

        load_unit(0)
        c_rows = consts.tile([P, PACK, H], BF16)
        nc.sync.dma_start(out=c_rows[:], in_=coefficients.rearrange("(i p) k -> p i k", p=P))
        for i in range(1, LOADS_AHEAD):
            load_unit(i)

        c_grouped = consts.tile([P, H, PACK], BF16, align_bytes=64)
        c_doubled = consts.tile([P, H, PACK], BF16, align_bytes=64)
        c_operand = {}

        def turn_coefficients():
            for half in range(PACK // UNIT_TILES):
                c_turned = psum_k3.tile([P, 2, UNIT_ROWS], F32, tag="k3")
                transpose_pairs(
                    nc, c_turned, identity,
                    [c_rows[:, half * UNIT_TILES + j, :] for j in range(UNIT_TILES)],
                )
                copy_pairs(nc, c_grouped[:, half * UNIT_ROWS : (half + 1) * UNIT_ROWS, :], c_turned)

        def double_coefficients():
            nc.vector.tensor_scalar_mul(out=c_doubled[:], in0=c_grouped[:], scalar1=2.0)

        def quantise_coefficients(weight):
            c_codes = consts.tile([P, H], U32, align_bytes=64, tag="c_codes%d" % weight)
            c_scales = consts.tile([P, H], U8, align_bytes=64, tag="c_scales%d" % weight)
            quantise(nc, c_codes[:], c_scales[:], (None, c_grouped, c_doubled)[weight][:])
            c_operand[weight] = (c_codes, c_scales)

        live = {}

        def unit_rows(tiles_sb, i):
            s, t0 = units[i]
            return tiles_sb[s][:, t0 : t0 + UNIT_TILES, :]

        def halve_k2(i):
            if shared(i):
                nc.vector.tensor_scalar_mul(
                    out=live["half_k2", i][:, 1, :], in0=unit_rows(k2_sb, i)[:, 1, :], scalar1=0.5
                )
                return
            half_k2 = work.tile([P, UNIT_TILES, H], BF16, tag="half_k2", bufs=4)
            nc.vector.tensor_scalar_mul(out=half_k2[:], in0=unit_rows(k2_sb, i), scalar1=0.5)
            live["half_k2", i] = half_k2

        def shared(i):
            return i % 2 == 0 and i > 3

        def scalar_halve(i):
            half_k2 = work.tile([P, UNIT_TILES, H], BF16, tag="half_k2", bufs=4)
            nc.scalar.activation(
                out=half_k2[:, 0, :], in_=unit_rows(k2_sb, i)[:, 0, :], func=COPY, scale=0.5
            )
            live["half_k2", i] = half_k2

        def add_a(i):
            a_rows = work.tile([P, UNIT_TILES, H], BF16)
            nc.vector.tensor_tensor(
                out=a_rows[:], in0=unit_rows(x_sb, i), in1=live["half_k2", i][:], op=ADD
            )
            live["a_rows", i] = a_rows

        def turn_a(i):
            a_turned = psum_a.tile([P, 2, UNIT_ROWS], F32)
            transpose_pairs(
                nc, a_turned, identity, [live["a_rows", i][:, j, :] for j in range(UNIT_TILES)]
            )
            live["a_turned", i] = a_turned

        def open_grouped(r):
            grouped = work.tile([P, 2 * UNIT_ROWS, PACK], BF16, align_bytes=64)
            live["grouped", r] = grouped

        def b_rows_grouped(i):
            return live["grouped", i + 3][:, :UNIT_ROWS, :]

        def a_rows_grouped(i):
            return live["grouped", i + 1][:, UNIT_ROWS:, :]

        def copy_a(i):
            copy_pairs(nc, a_rows_grouped(i), live["a_turned", i])

        def quantise_round(r):
            first = 0 if in_flight(r - 3) else UNIT_ROWS
            end = 2 * UNIT_ROWS if in_flight(r - 1) else UNIT_ROWS
            codes = lasting.tile([P, 2 * UNIT_ROWS], U32, align_bytes=64)
            scales = lasting.tile([P, 2 * UNIT_ROWS], U8, align_bytes=64)
            quantise(
                nc, codes[:, first:end], scales[:, first:end], live["grouped", r][:, first:end, :]
            )
            live["b", r - 3] = (codes, scales, 0)
            live["a", r - 1] = (codes, scales, UNIT_ROWS)

        def product(acc, rows_operand, j, weight, start, stop):
            codes, scales, first_row = rows_operand
            tile_rows = slice(first_row + j * P, first_row + (j + 1) * P)
            c_codes, c_scales = c_operand[weight]
            nc.tensor.matmul_mx(
                out=acc[:],
                lhsT=codes[:, tile_rows].bitcast(FP8X4),
                lhsT_scale=scales[:, tile_rows],
                rhs=c_codes[:].bitcast(FP8X4),
                rhs_scale=c_scales[:],
                start=start,
                stop=stop,
            )

        def first_product(i, j):
            k3 = psum_k3.tile([P, H], F32, tag="k3")
            product(k3, live["a", i], j, 1, True, True)
            live["k3", i, j] = k3

        def widen(i, j, name, rows):
            wide = lasting.tile([P, PACK, P], F32, tag=name, bufs=8)
            nc.scalar.copy(
                out=wide[:].rearrange("p (u e) q -> p u e q", u=2), in_=by_word_value(rows)
            )
            live[name, i, j] = wide

        def widen_y(i, j):
            widen(i, j, "y_wide", unit_rows(x_sb, i)[:, j, :])

        def widen_k3(i, j):
            widen(i, j, "k3_wide", live["k3", i, j][:])

        def turn_b(i, j):
            b_turned = psum_b.tile([P, PACK, P], F32)
            for t in range(PACK):
                for name, first in (("y_wide", True), ("k3_wide", False)):
                    nc.tensor.matmul(
                        out=b_turned[:, t, :],
                        lhsT=live[name, i, j][:, t, :],
                        rhs=identity[:],
                        start=first,
                        stop=not first,
                        is_transpose=True,
                    )
            live["b_turned", i, j] = b_turned

        def round_b(i, j):
            nc.scalar.copy(
                out=b_rows_grouped(i)[:, tiles[j], :],
                in_=live["b_turned", i, j][:].rearrange("p t n -> p n t"),
            )

        def second_product(i, j):
            stages = psum_sum.tile([P, H], F32, tag="sum")
            product(stages, live["a", i], j, 2, True, False)
            product(stages, live["b", i], j, 1, False, True)
            live["stages", i, j] = stages

        def rest_difference(i):
            open_rest(i)
            if i == 0:
                difference(nc.vector, i, 0, H)
                difference(nc.vector, i, H, UNIT_TILES * H)
            else:
                difference(nc.vector, i, taken.get(i, 0), UNIT_TILES * H)

        taken = {TENSOR_COLUMNS_UNIT: TENSOR_COLUMNS}

        def open_rest(i):
            if ("rest", i) not in live:
                rest = lasting.tile([P, UNIT_TILES, H], F32, tag="rest", bufs=9)
                live["rest", i] = rest

        def difference(engine, i, first, end):
            s, t0 = units[i]
            flat = [
                x_sb[s][:, t : t + UNIT_TILES, :].rearrange("p t h -> p (t h)")[:, first:end]
                for t in (t0, t0 + 1)
            ]
            engine.tensor_tensor(
                out=live["rest", i][:].rearrange("p t h -> p (t h)")[:, first:end],
                in0=flat[0], in1=flat[1], op=SUBTRACT,
            )

        def gpsimd_difference(i, after):
            nc.gpsimd.tensor_copy(out=started[:], in_=after[:, UNIT_TILES - 1, H - 2 : H])
            open_rest(i)
            first = taken.get(i, 0)
            taken[i] = first + GPSIMD_COLUMNS
            difference(nc.gpsimd, i, first, first + GPSIMD_COLUMNS)

        def rest_add(i, stage_sb, weight):
            first = TENSOR_COLUMNS if i == TENSOR_COLUMNS_UNIT else 0
            rest = live["rest", i][:].rearrange("p t h -> p (t h)")[:, first:]
            rows = unit_rows(stage_sb, i).rearrange("p t h -> p (t h)")[:, first:]
            nc.vector.scalar_tensor_tensor(
                out=rest, in0=rows, scalar=weight, in1=rest, op0=MULT, op1=ADD
            )

        def tensor_rest(i, j, columns=slice(0, H)):
            s, t0 = units[i]
            t = t0 + j
            terms = (
                (6.0, x_sb[s][:, t, :]),
                (-6.0, x_sb[s][:, t + 1, :]),
                (2.0, k2_sb[s][:, t, :]),
                (1.0, k1_sb[s][:, t, :]),
            )
            six_rest = psum_k3.tile([P, H], F32, tag="k3")
            for n, (weight, rows) in enumerate(terms):
                nc.tensor.matmul(
                    out=six_rest[:, columns], lhsT=weighted[weight][:], rhs=rows[:, columns],
                    start=n == 0, stop=n == len(terms) - 1,
                )
            live["six_rest", i, j] = six_rest

        def copy_tensor_rest(i, j, columns=slice(0, H)):
            open_rest(i)
            nc.scalar.activation(
                out=live["rest", i][:, j, columns], in_=live["six_rest", i, j][:, columns],
                func=COPY, scale=1.0 / 6.0,
            )

        vector_rest_units = [i for i in range(len(units)) if i not in TENSOR_REST_UNITS]
        tensor_rest_tiles = [(i, j) for i in TENSOR_REST_UNITS for j in range(UNIT_TILES)]

        def rest_step(k):
            n, step = divmod(k, REST_STEPS)
            i = vector_rest_units[n]
            if step == 0:
                rest_difference(i)
            elif step == 1:
                rest_add(i, k2_sb, 1.0 / 3.0)
            else:
                rest_add(i, k1_sb, 1.0 / 6.0)

        def finish(i, j, columns=slice(0, H)):
            rest = live["rest", i]
            nc.vector.scalar_tensor_tensor(
                out=rest[:, j, columns], in0=live["stages", i, j][:, columns], scalar=1.0 / 6.0,
                in1=rest[:, j, columns], op0=MULT, op1=ADD,
            )

        def store(i, j, columns=slice(0, H)):
            s, t0 = units[i]
            nc.sync.dma_start(
                out=out[s].rearrange("(p t) h -> p t h", t=STATES_PER_PARTITION)[:, t0 + j, columns],
                in_=live["rest", i][:, j, columns],
            )

        def in_flight(i):
            return 0 <= i < len(units)

        rounds = len(units) + STAGES_AFTER_A
        all_rest_steps = REST_STEPS * len(vector_rest_units)

        def rest_steps_of(r):
            return list(
                range(
                    (r * all_rest_steps + rounds - 1) // rounds,
                    ((r + 1) * all_rest_steps + rounds - 1) // rounds,
                )
            )

        def finish_and_store(i, j, columns=slice(0, H)):
            finish(i, j, columns)
            store(i, j, columns)

        def pipeline_round(r):
            rest_steps = rest_steps_of(r)
            if r == 0:
                rest_steps = rest_steps[2:]
            if in_flight(r + LOADS_AHEAD):
                load_unit(r + LOADS_AHEAD)
            first, second = range(UNIT_TILES)
            if in_flight(r - 2):
                turn_b(r - 2, first)
            if in_flight(r):
                turn_a(r)
            if in_flight(r - 3) or in_flight(r - 1):
                quantise_round(r)
            if in_flight(r - 3):
                second_product(r - 3, first)
            if in_flight(r - 1):
                first_product(r - 1, first)
            if in_flight(r - 2) or in_flight(r):
                open_grouped(r + 1)
            if in_flight(r - 2):
                turn_b(r - 2, second)
                round_b(r - 2, first)
            if in_flight(r):
                copy_a(r)
            rest_step(rest_steps[0])
            if r >= len(units):
                finish_and_store(r - 4, second)
            if in_flight(r + 1):
                halve_k2(r + 1)
            if in_flight(r - 1):
                widen_k3(r - 1, first)
            if in_flight(r + 2) and shared(r + 2):
                scalar_halve(r + 2)
            if in_flight(r - 2):
                round_b(r - 2, second)
            if in_flight(r - 3):
                second_product(r - 3, second)
            if in_flight(r - 1):
                first_product(r - 1, second)
            if 0 <= r - 1 < 2 * len(tensor_rest_tiles) and (r - 1) % 2 == 0:
                tensor_rest(*tensor_rest_tiles[(r - 1) // 2])
            if r == TENSOR_COLUMNS_UNIT:
                tensor_rest(r, 0, slice(0, TENSOR_COLUMNS))
            for k in rest_steps[1:]:
                rest_step(k)
            if in_flight(r - 1):
                widen_k3(r - 1, second)
            if in_flight(r + 1):
                widen_y(r + 1, first)
            if in_flight(r + 1):
                widen_y(r + 1, second)
            if 0 <= r - 1 < 2 * len(tensor_rest_tiles) and (r - 1) % 2 == 0:
                copy_tensor_rest(*tensor_rest_tiles[(r - 1) // 2])
            if r == TENSOR_COLUMNS_UNIT:
                copy_tensor_rest(r, 0, slice(0, TENSOR_COLUMNS))
            if in_flight(r - 4) and r < len(units):
                n = r if r < len(vector_rest_units) else r - 3
                last_rest = live["rest", vector_rest_units[rest_steps[-1] // REST_STEPS]]
                gpsimd_difference(vector_rest_units[n], last_rest)
            if in_flight(r + 1):
                add_a(r + 1)
            if in_flight(r - 3):
                finish_and_store(r - 3, first)
            if in_flight(r - 4) and r < len(units):
                finish_and_store(r - 4, second)

        for j in range(UNIT_TILES):
            widen_y(0, j)
        rest_step(rest_steps_of(0)[0])
        halve_k2(0)
        rest_step(rest_steps_of(0)[1])
        add_a(0)
        turn_coefficients()
        pipeline_round(0)
        quantise_coefficients(1)
        pipeline_round(1)
        double_coefficients()
        pipeline_round(2)
        quantise_coefficients(2)
        for r in range(3, rounds):
            pipeline_round(r)
        for half in range(2):
            columns = slice(half * H // 2, (half + 1) * H // 2)
            finish_and_store(len(units) - 1, UNIT_TILES - 1, columns)
